import numpy as np
import ml_dtypes


def mxq(x, axis, fmt="e4m3"):
    dtype, down = {"e4m3": (ml_dtypes.float8_e4m3fn, 7), "e5m2": (ml_dtypes.float8_e5m2, 14)}[fmt]
    v = np.moveaxis(np.asarray(x, np.float32).astype(ml_dtypes.bfloat16).astype(np.float64), axis, -1)
    blocks = v.reshape(v.shape[:-1] + (-1, 32))
    amax = np.abs(blocks).max(-1, keepdims=True)
    byte = np.maximum(np.where(amax > 0, np.frexp(amax)[1] - 1 + 127, 0) - down, 1)
    scale = np.exp2(byte - 127.0)
    codes = (blocks / scale).astype(np.float32).astype(dtype).astype(np.float64)
    return np.moveaxis((codes * scale).reshape(v.shape), -1, axis)


WIDE = False


def mx_kscale(k):
    if not WIDE:
        return np.ones(k)
    levels = np.array([10, -10, 5, -5, 0])
    if k % 512:
        return np.exp2(np.random.permutation(np.resize(levels, k // 32))).repeat(32)
    a = np.empty((k // 512, 16))
    for p in range(k // 512):
        a[p, :8] = np.random.permutation(np.resize(levels, 8))
        for g in range(8):
            far = levels[np.abs(levels - a[p, g]) >= 10]
            a[p, g + 8] = far[np.random.randint(len(far))]
    return np.exp2(a.ravel()).repeat(32)


BF16 = ml_dtypes.bfloat16


def bf(x):
    return np.asarray(x, np.float32).astype(BF16)


def f64(x):
    return np.asarray(x).astype(np.float64)


B, L, H, G, DEPTH = 64, 64, 1024, 256, 3
EPS = 1e-5


def layernorm(v, g, b):
    mu = v.mean(-1, keepdims=True)
    var = np.square(v - mu).mean(-1, keepdims=True)
    return (v - mu) / np.sqrt(var + EPS) * g + b


def setup_inputs():
    s, t = mx_kscale(H), mx_kscale(H)
    return {"x_nodes": bf(np.random.standard_normal((B, L, H)) * s),
            "w1": bf(np.random.standard_normal((H, H)) / np.sqrt(H) / s[:, None]),
            "b1": bf(np.random.standard_normal(H) * 0.3),
            "gamma": bf((1.0 + 0.1 * np.random.standard_normal(H)) * t),
            "beta": bf(0.2 * np.random.standard_normal(H) * t),
            "w2": bf(np.random.standard_normal((H, G)) / np.sqrt(H) / t[:, None]),
            "b2": bf(np.random.standard_normal(G) * 0.3)}


def reference(x_nodes, w1, b1, gamma, beta, w2, b2):
    h = (mxq(f64(x_nodes), 2, "e4m3") @ mxq(f64(w1), 0, "e4m3")) + f64(b1)
    r = np.maximum(layernorm(h, f64(gamma), f64(beta)), 0.0)
    x1 = (mxq(r, 2, "e4m3") @ mxq(f64(w2), 0, "e4m3")) + f64(b2)
    x2 = np.broadcast_to(x1.max(axis=1, keepdims=True), x1.shape)
    x = np.concatenate([x1, x2], axis=2)
    return x.max(axis=1)

@@ -1,0 +1,420 @@
+from contextlib import ExitStack
+
+import concourse.mybir as mybir
+from concourse.masks import make_identity
+
+F32 = mybir.dt.float32
+BF16 = mybir.dt.bfloat16
+U32 = mybir.dt.uint32
+U8 = mybir.dt.uint8
+FP8X4 = mybir.dt.float8_e4m3fn_x4
+ACT = mybir.ActivationFunctionType
+ALU = mybir.AluOpType
+AX = mybir.AxisListType
+
+P = 128
+PACK = 4
+K_PASS = P * PACK
+BANK = 512
+
+TOKENS = 64 * 64
+NODES = 64
+H = 1024
+G = 256
+EPS = 1e-5
+PASSES = H // K_PASS
+TILES = 2
+BLOCK = TILES * P
+N_BLOCKS = TOKENS // BLOCK
+LINES = BLOCK // NODES
+CHUNKS = H // P
+HALVES = H // BANK
+CHUNKS_PER_BANK = BANK // BLOCK
+T_BANKS = CHUNKS // CHUNKS_PER_BANK
+G_TILES = G // P
+
+LAG_DEVIATION = 1
+LAG_NORMALISE = 2
+LAG_TRANSPOSE = 3
+LAG_READ_OUT = 4
+X_AHEAD = 2
+LOAD_AHEAD = 4
+
+FLOPS = 2 * TOKENS * H * H + 2 * TOKENS * H * G
+
+
+def regroup(nc, grouped, planes):
+    nc.vector.tensor_copy(
+        out=grouped.rearrange("p (c i) t -> p c t i", i=4),
+        in_=planes.rearrange("p t (c i) -> p c t i", i=4),
+    )
+
+
+def tile_sub_graph_pb_t_kernel(tc, x_nodes, w1, b1, gamma, beta, w2, b2, out):
+    nc = tc.nc
+    x = x_nodes.rearrange("b l k -> (b l) k")
+
+    with ExitStack() as ctx:
+        const = ctx.enter_context(tc.tile_pool(name="const", bufs=1))
+        wstage = ctx.enter_context(tc.tile_pool(name="wstage", bufs=2))
+        xpool = ctx.enter_context(tc.tile_pool(name="xpool", bufs=2))
+        hpool = ctx.enter_context(tc.tile_pool(name="hpool", bufs=5))
+        stat = ctx.enter_context(tc.tile_pool(name="stat", bufs=4))
+        rpool = ctx.enter_context(tc.tile_pool(name="rpool", bufs=2))
+        psum = ctx.enter_context(tc.psum_pool(name="psum", bufs=1))
+        ctx.enter_context(tc.manual_schedule())
+
+        def in_range(blk):
+            return 0 <= blk < N_BLOCKS
+
+        w1_raws = {}
+        for g in range(PASSES):
+            w1_raw = wstage.tile([P, PACK, H], BF16, tag="w1_raw")
+            for n in range(HALVES):
+                cols_n = slice(n * BANK, (n + 1) * BANK)
+                nc.sync.dma_start(
+                    out=w1_raw[:, :, cols_n],
+                    in_=w1[K_PASS * g : K_PASS * (g + 1), cols_n].rearrange(
+                        "(p t) c -> p t c", t=PACK
+                    ),
+                )
+            w1_raws[g] = w1_raw
+
+        x_sbs = {}
+
+        def load_x(blk):
+            if not in_range(blk):
+                return
+            x_sb = xpool.tile([P, TILES * H], BF16, tag="x_sb", bufs=LOAD_AHEAD)
+            nc.sync.dma_start(
+                out=x_sb[:].rearrange("p (i k) -> p i k", i=TILES),
+                in_=x[blk * BLOCK : (blk + 1) * BLOCK, :].rearrange("(i p) k -> p i k", p=P),
+            )
+            x_sbs[blk] = x_sb
+
+        load_x(0)
+        load_x(1)
+        w2_raw = const.tile([P, PASSES, PACK, G], BF16)
+        nc.sync.dma_start(
+            out=w2_raw[:], in_=w2.rearrange("(g p j) n -> p g j n", p=P, j=PACK)
+        )
+        for blk in range(2, LOAD_AHEAD):
+            load_x(blk)
+
+        gamma_raw = const.tile([P, PASSES, PACK], BF16)
+        nc.scalar.dma_start(
+            out=gamma_raw[:], in_=gamma.rearrange("(g p j) -> p g j", p=P, j=PACK)
+        )
+        beta_raw = const.tile([P, PASSES, PACK], BF16)
+        nc.scalar.dma_start(
+            out=beta_raw[:], in_=beta.rearrange("(g p j) -> p g j", p=P, j=PACK)
+        )
+        rows = const.tile([P, P], BF16)
+        nc.vector.memset(rows[:], 0.0)
+        nc.scalar.dma_start(out=rows[0:G_TILES, :], in_=b2.rearrange("(c p) -> c p", p=P))
+        b1_row = const.tile([P, H], BF16)
+        nc.vector.memset(b1_row[:], 0.0)
+        nc.scalar.dma_start(out=b1_row[0:1, :], in_=b1.rearrange("(o h) -> o h", o=1))
+
+        ident = const.tile([P, P], F32)
+        make_identity(nc, ident[:])
+        eps_col = const.tile([P, 1], F32)
+        nc.vector.memset(eps_col[:], EPS)
+        ones = const.tile([P, P], BF16)
+        nc.vector.memset(ones[:], 1.0)
+        warm = const.tile([P, 1], F32)
+        nc.scalar.activation(out=warm[:], in_=eps_col[:], func=ACT.Sqrt)
+
+        rows_f32 = const.tile([P, P], F32)
+        nc.vector.tensor_copy(out=rows_f32[:], in_=rows[:])
+        cols_ps = psum.tile([P, P], F32, tag="xT", bufs=1)
+        nc.tensor.transpose(cols_ps[:], rows_f32[:], ident[:])
+        b2_col = const.tile([P, G_TILES], F32)
+        nc.vector.tensor_copy(out=b2_col[:], in_=cols_ps[:, 0:G_TILES])
+        gamma_col = const.tile([P, CHUNKS], F32)
+        nc.vector.tensor_copy(out=gamma_col[:], in_=gamma_raw[:].rearrange("p g j -> p (g j)"))
+        beta_col = const.tile([P, CHUNKS], F32)
+        nc.vector.tensor_copy(out=beta_col[:], in_=beta_raw[:].rearrange("p g j -> p (g j)"))
+
+        b1_all = const.tile([P, H], F32)
+        for n in range(HALVES):
+            b1_ps = psum.tile([P, BANK], F32, tag="h_ps", bufs=4)
+            nc.tensor.matmul(
+                out=b1_ps[:], lhsT=ones[:], rhs=b1_row[:, n * BANK : (n + 1) * BANK],
+                start=True, stop=True,
+            )
+            nc.scalar.copy(
+                out=b1_all[:, n * BANK : (n + 1) * BANK].rearrange("p (j m) -> p j m", j=PACK),
+                in_=b1_ps[:].rearrange("p (m j) -> p j m", j=PACK),
+            )
+
+        node_max = const.tile([P, G_TILES, TOKENS // NODES], F32)
+
+        x_grps = {}
+        x_mx = {}
+
+        def transpose_x(blk, i):
+            if not in_range(blk):
+                return
+            if i == 0:
+                x_grp = xpool.tile([P, TILES * H], BF16, tag="x_grp", align_bytes=64)
+                x_grps[blk] = x_grp
+            x_words = x_sbs[blk][:].bitcast(F32)
+            x_grp_words = x_grps[blk][:].bitcast(F32)
+            xT_ps = psum.tile([P, PACK, P], F32, tag="xT", bufs=1)
+            for q in range(PACK):
+                g, u = divmod(q, 2)
+                w0 = i * (H // 2) + g * 2 * P
+                nc.tensor.transpose(xT_ps[:, q, :], x_words[:, w0 + u : w0 + 2 * P : 2], ident[:])
+            nc.scalar.copy(
+                out=x_grp_words[:, i * (H // 2) : (i + 1) * (H // 2)].rearrange(
+                    "p (g w u) -> p g w u", g=PASSES, u=2
+                ),
+                in_=xT_ps[:].rearrange("p (g u) w -> p g w u", g=PASSES),
+            )
+
+        def quantise_x(blk):
+            if not in_range(blk):
+                return
+            x_codes = xpool.tile([P, TILES, PASSES, P], U32, tag="x_codes", align_bytes=64)
+            x_scales = xpool.tile([P, TILES, PASSES, P], U8, tag="x_scales", align_bytes=64)
+            nc.vector.quantize_mx(
+                out=x_codes[:].rearrange("p i g w -> p (i g w)").bitcast(FP8X4),
+                scales=x_scales[:].rearrange("p i g w -> p (i g w)"),
+                in_=x_grps[blk][:],
+            )
+            x_mx[blk] = (x_codes, x_scales)
+
+        h_pss = {}
+        h_sbs = {}
+        neg_means = {}
+        sq_sums = {}
+        stds = {}
+
+        def first_matmul(blk, i, n):
+            if not in_range(blk):
+                return
+            x_codes, x_scales = x_mx[blk]
+            cols_n = slice(n * BANK, (n + 1) * BANK)
+            h_ps = psum.tile([P, BANK], F32, tag="h_ps", bufs=4)
+            for g in range(PASSES):
+                nc.tensor.matmul_mx(
+                    out=h_ps[:],
+                    lhsT=x_codes[:, i, g, :].bitcast(FP8X4),
+                    lhsT_scale=x_scales[:, i, g, :],
+                    rhs=w1_codes[:, g, cols_n].bitcast(FP8X4),
+                    rhs_scale=w1_scales[:, g, cols_n],
+                    start=(g == 0),
+                    stop=(g == PASSES - 1),
+                )
+            h_pss[(blk, i, n)] = h_ps
+
+        def add_bias(blk):
+            if not in_range(blk):
+                return
+            h_sb = hpool.tile([P, TILES, H], F32, tag="h_sb")
+            h_sum = stat.tile([P, TILES, HALVES], F32, tag="h_sum")
+            neg_mean = stat.tile([P, TILES], F32, tag="neg_mean")
+            for i in range(TILES):
+                for n in range(HALVES):
+                    cols_n = slice(n * BANK, (n + 1) * BANK)
+                    nc.vector.scalar_tensor_tensor(
+                        out=h_sb[:, i, cols_n].rearrange("p (j m) -> p j m", j=PACK),
+                        in0=h_pss[(blk, i, n)][:].rearrange("p (m j) -> p j m", j=PACK),
+                        scalar=1.0,
+                        in1=b1_all[:, cols_n].rearrange("p (j m) -> p j m", j=PACK),
+                        op0=ALU.mult,
+                        op1=ALU.add,
+                        accum_out=h_sum[:, i, n : n + 1],
+                    )
+                nc.vector.tensor_scalar(
+                    out=neg_mean[:, i : i + 1],
+                    in0=h_sum[:, i, 0:1],
+                    scalar1=h_sum[:, i, 1:2],
+                    scalar2=-1.0 / H,
+                    op0=ALU.add,
+                    op1=ALU.mult,
+                )
+            h_sbs[blk] = h_sb
+            neg_means[blk] = neg_mean
+
+        def squared_deviations(blk, i):
+            if not in_range(blk):
+                return
+            if i == 0:
+                sq_sum = stat.tile([P, TILES], F32, tag="sq_sum")
+                sq_sums[blk] = sq_sum
+            squares = hpool.tile([P, H], BF16, tag="squares", bufs=2)
+            nc.scalar.activation(
+                out=squares[:],
+                in_=h_sbs[blk][:, i, :],
+                func=ACT.Square,
+                bias=neg_means[blk][:, i : i + 1],
+                scale=1.0,
+                accum_out=sq_sums[blk][:, i : i + 1],
+            )
+
+        def standard_deviation(blk):
+            if not in_range(blk):
+                return
+            std = stat.tile([P, TILES], F32, tag="std")
+            nc.scalar.activation(
+                out=std[:], in_=sq_sums[blk][:], func=ACT.Sqrt, bias=eps_col[:, 0:1],
+                scale=1.0 / H,
+            )
+            stds[blk] = std
+
+        def normalise(blk):
+            if not in_range(blk):
+                return
+            rstd = stat.tile([P, TILES], F32, tag="rstd")
+            nc.vector.reciprocal(out=rstd[:], in_=stds[blk][:])
+            for i in range(TILES):
+                nc.gpsimd.tensor_scalar(
+                    out=h_sbs[blk][:, i, :],
+                    in0=h_sbs[blk][:, i, :],
+                    scalar1=neg_means[blk][:, i : i + 1],
+                    scalar2=rstd[:, i : i + 1],
+                    op0=ALU.add,
+                    op1=ALU.mult,
+                )
+
+        r_planess = {}
+        r_grps = {}
+        r_mx = {}
+
+        def transpose_and_activate(blk, bank):
+            if not in_range(blk):
+                return
+            if bank == 0:
+                r_planes = rpool.tile([P, CHUNKS, BLOCK], BF16, tag="r_planes")
+                r_planess[blk] = r_planes
+            nT_ps = psum.tile([P, CHUNKS_PER_BANK, BLOCK], F32, tag="nT", bufs=2)
+            for s in range(CHUNKS_PER_BANK):
+                c = bank * CHUNKS_PER_BANK + s
+                for i in range(TILES):
+                    nc.tensor.transpose(
+                        nT_ps[:, s, i * P : (i + 1) * P],
+                        h_sbs[blk][:, i, c * P : (c + 1) * P],
+                        ident[:],
+                    )
+            for s in range(CHUNKS_PER_BANK):
+                c = bank * CHUNKS_PER_BANK + s
+                nc.scalar.activation(
+                    out=r_planess[blk][:, c, :],
+                    in_=nT_ps[:, s, :],
+                    func=ACT.Relu,
+                    bias=beta_col[:, c : c + 1],
+                    scale=gamma_col[:, c : c + 1],
+                )
+
+        def quantise_r(blk):
+            if not in_range(blk):
+                return
+            r_grp = rpool.tile([P, PASSES, BLOCK, PACK], BF16, tag="r_grp", align_bytes=64)
+            r_codes = rpool.tile([P, PASSES, BLOCK], U32, tag="r_codes", align_bytes=64)
+            r_scales = rpool.tile([P, PASSES, BLOCK], U8, tag="r_scales", align_bytes=64)
+            for g in range(PASSES):
+                regroup(nc, r_grp[:, g, :, :], r_planess[blk][:, PACK * g : PACK * (g + 1), :])
+            for g in range(PASSES):
+                nc.vector.quantize_mx(
+                    out=r_codes[:, g, :].bitcast(FP8X4),
+                    scales=r_scales[:, g, :],
+                    in_=r_grp[:, g, :, :].rearrange("p w j -> p (w j)"),
+                )
+            r_mx[blk] = (r_codes, r_scales)
+
+        x1_pss = {}
+
+        def second_matmul(blk):
+            if not in_range(blk):
+                return
+            r_codes, r_scales = r_mx[blk]
+            x1_ps = psum.tile([P, G_TILES, BLOCK], F32, tag="x1", bufs=1)
+            for cc in range(G_TILES):
+                for g in range(PASSES):
+                    nc.tensor.matmul_mx(
+                        out=x1_ps[:, cc, :],
+                        lhsT=w2_codes[:, g, cc * P : (cc + 1) * P].bitcast(FP8X4),
+                        lhsT_scale=w2_scales[:, g, cc * P : (cc + 1) * P],
+                        rhs=r_codes[:, g, :].bitcast(FP8X4),
+                        rhs_scale=r_scales[:, g, :],
+                        start=(g == 0),
+                        stop=(g == PASSES - 1),
+                    )
+            x1_pss[blk] = x1_ps
+
+        def node_maxima(blk):
+            if not in_range(blk):
+                return
+            nc.vector.tensor_reduce(
+                out=node_max[:, :, blk * LINES : (blk + 1) * LINES],
+                in_=x1_pss[blk][:].rearrange("p c (q l) -> p c q l", l=NODES),
+                axis=AX.X,
+                op=ALU.max,
+            )
+
+        for blk in range(X_AHEAD):
+            for i in range(TILES):
+                transpose_x(blk, i)
+
+        w1_codes = const.tile([P, PASSES, H], U32, align_bytes=64)
+        w1_scales = const.tile([P, PASSES, H], U8, align_bytes=64)
+        for g in range(PASSES):
+            w1_grps = {}
+            for n in range(HALVES):
+                w1_grp = wstage.tile([P, BANK, PACK], BF16, tag="w1_grp", align_bytes=64)
+                regroup(nc, w1_grp[:], w1_raws[g][:, :, n * BANK : (n + 1) * BANK])
+                w1_grps[n] = w1_grp
+            for n in range(HALVES):
+                cols_n = slice(n * BANK, (n + 1) * BANK)
+                nc.vector.quantize_mx(
+                    out=w1_codes[:, g, cols_n].bitcast(FP8X4),
+                    scales=w1_scales[:, g, cols_n],
+                    in_=w1_grps[n][:].rearrange("p c t -> p (c t)"),
+                )
+        quantise_x(0)
+
+        w2_grp = const.tile([P, PASSES, G, PACK], BF16, align_bytes=64)
+        w2_codes = const.tile([P, PASSES, G], U32, align_bytes=64)
+        w2_scales = const.tile([P, PASSES, G], U8, align_bytes=64)
+        for g in range(PASSES):
+            regroup(nc, w2_grp[:, g, :, :], w2_raw[:, g, :, :])
+        nc.vector.quantize_mx(
+            out=w2_codes[:].rearrange("p g c -> p (g c)").bitcast(FP8X4),
+            scales=w2_scales[:].rearrange("p g c -> p (g c)"),
+            in_=w2_grp[:].rearrange("p g c t -> p (g c t)"),
+        )
+
+        for step in range(N_BLOCKS + LAG_READ_OUT):
+            load_x(step + LOAD_AHEAD)
+            quantise_x(step + 1)
+            quantise_r(step - LAG_READ_OUT)
+            normalise(step - LAG_NORMALISE)
+            for i in range(TILES):
+                for n in range(HALVES):
+                    first_matmul(step, i, n)
+                squared_deviations(step - LAG_DEVIATION, i)
+                for n in range(HALVES):
+                    transpose_and_activate(step - LAG_TRANSPOSE, i * HALVES + n)
+                transpose_x(step + X_AHEAD, i)
+            second_matmul(step - LAG_READ_OUT)
+            standard_deviation(step - LAG_DEVIATION)
+            add_bias(step)
+            node_maxima(step - LAG_READ_OUT)
+
+        for cc in range(G_TILES):
+            nc.vector.tensor_scalar_add(
+                out=node_max[:, cc, :], in0=node_max[:, cc, :], scalar1=b2_col[:, cc : cc + 1]
+            )
+        maxT_ps = psum.tile([P, P], F32, tag="xT", bufs=1)
+        nc.tensor.transpose(maxT_ps[:], node_max[:].rearrange("p c b -> p (c b)"), ident[:])
+        result = const.tile([P, 2, P], F32)
+        for rep in range(2):
+            nc.vector.tensor_copy(out=result[:, rep, :], in_=maxT_ps[:])
+        out_view = out.rearrange("b (r c j) -> c b r j", r=2, c=G_TILES)
+        n_lines = TOKENS // NODES
+        for cc in range(G_TILES):
+            nc.sync.dma_start(
+                out=out_view[cc], in_=result[cc * n_lines : (cc + 1) * n_lines, :, :]
+            )

@@ -19,26 +19,19 @@ BANK = 512
 
 TOKENS = 64 * 64
 NODES = 64
+LINES = TOKENS // NODES
 H = 1024
 G = 256
 EPS = 1e-5
 PASSES = H // K_PASS
-TILES = 2
-BLOCK = TILES * P
-N_BLOCKS = TOKENS // BLOCK
-LINES = BLOCK // NODES
-CHUNKS = H // P
+N_TILES = TOKENS // P
 HALVES = H // BANK
-CHUNKS_PER_BANK = BANK // BLOCK
-T_BANKS = CHUNKS // CHUNKS_PER_BANK
 G_TILES = G // P
+PAIR = 2
+PAIR_LINES = PAIR * P // NODES
 
-LAG_DEVIATION = 1
-LAG_NORMALISE = 2
-LAG_TRANSPOSE = 3
-LAG_READ_OUT = 4
-X_AHEAD = 2
-LOAD_AHEAD = 4
+X_AHEAD = 3
+LOAD_AHEAD = 8
 
 FLOPS = 2 * TOKENS * H * H + 2 * TOKENS * H * G
 
@@ -57,50 +50,47 @@ def tile_sub_graph_pb_t_kernel(tc, x_nodes, w1, b1, gamma, beta, w2, b2, out):
     with ExitStack() as ctx:
         const = ctx.enter_context(tc.tile_pool(name="const", bufs=1))
         wstage = ctx.enter_context(tc.tile_pool(name="wstage", bufs=2))
-        xpool = ctx.enter_context(tc.tile_pool(name="xpool", bufs=2))
-        hpool = ctx.enter_context(tc.tile_pool(name="hpool", bufs=5))
+        xpool = ctx.enter_context(tc.tile_pool(name="xpool", bufs=3))
+        hpool = ctx.enter_context(tc.tile_pool(name="hpool", bufs=4))
         stat = ctx.enter_context(tc.tile_pool(name="stat", bufs=4))
         rpool = ctx.enter_context(tc.tile_pool(name="rpool", bufs=2))
         psum = ctx.enter_context(tc.psum_pool(name="psum", bufs=1))
         ctx.enter_context(tc.manual_schedule())
 
-        def in_range(blk):
-            return 0 <= blk < N_BLOCKS
-
-        w1_raws = {}
-        for g in range(PASSES):
-            w1_raw = wstage.tile([P, PACK, H], BF16, tag="w1_raw")
-            for n in range(HALVES):
-                cols_n = slice(n * BANK, (n + 1) * BANK)
-                nc.sync.dma_start(
-                    out=w1_raw[:, :, cols_n],
-                    in_=w1[K_PASS * g : K_PASS * (g + 1), cols_n].rearrange(
-                        "(p t) c -> p t c", t=PACK
-                    ),
-                )
-            w1_raws[g] = w1_raw
+        def in_range(i):
+            return 0 <= i < N_TILES
 
         x_sbs = {}
 
-        def load_x(blk):
-            if not in_range(blk):
+        def load_x(i):
+            if not in_range(i):
                 return
-            x_sb = xpool.tile([P, TILES * H], BF16, tag="x_sb", bufs=LOAD_AHEAD)
+            x_sb = xpool.tile([P, H], BF16, tag="x_sb", bufs=LOAD_AHEAD)
+            nc.sync.dma_start(out=x_sb[:], in_=x[i * P : (i + 1) * P, :])
+            x_sbs[i] = x_sb
+
+        w1_raws = {}
+
+        def load_w1(g, n):
+            w1_raw = const.tile([P, PACK, BANK], BF16, name=f"w1_raw_{g}_{n}")
             nc.sync.dma_start(
-                out=x_sb[:].rearrange("p (i k) -> p i k", i=TILES),
-                in_=x[blk * BLOCK : (blk + 1) * BLOCK, :].rearrange("(i p) k -> p i k", p=P),
+                out=w1_raw[:],
+                in_=w1[K_PASS * g : K_PASS * (g + 1), n * BANK : (n + 1) * BANK].rearrange(
+                    "(p t) c -> p t c", t=PACK
+                ),
             )
-            x_sbs[blk] = x_sb
+            w1_raws[(g, n)] = w1_raw
 
+        b1_row = const.tile([P, H], BF16)
+        nc.vector.memset(b1_row[:], 0.0)
+        load_w1(0, 0)
         load_x(0)
+        load_w1(1, 0)
         load_x(1)
-        w2_raw = const.tile([P, PASSES, PACK, G], BF16)
-        nc.sync.dma_start(
-            out=w2_raw[:], in_=w2.rearrange("(g p j) n -> p g j n", p=P, j=PACK)
-        )
-        for blk in range(2, LOAD_AHEAD):
-            load_x(blk)
-
+        load_w1(0, 1)
+        load_x(2)
+        load_w1(1, 1)
+        nc.scalar.dma_start(out=b1_row[0:1, :], in_=b1.rearrange("(o h) -> o h", o=1))
         gamma_raw = const.tile([P, PASSES, PACK], BF16)
         nc.scalar.dma_start(
             out=gamma_raw[:], in_=gamma.rearrange("(g p j) -> p g j", p=P, j=PACK)
@@ -109,32 +99,33 @@ def tile_sub_graph_pb_t_kernel(tc, x_nodes, w1, b1, gamma, beta, w2, b2, out):
         nc.scalar.dma_start(
             out=beta_raw[:], in_=beta.rearrange("(g p j) -> p g j", p=P, j=PACK)
         )
-        rows = const.tile([P, P], BF16)
-        nc.vector.memset(rows[:], 0.0)
-        nc.scalar.dma_start(out=rows[0:G_TILES, :], in_=b2.rearrange("(c p) -> c p", p=P))
-        b1_row = const.tile([P, H], BF16)
-        nc.vector.memset(b1_row[:], 0.0)
-        nc.scalar.dma_start(out=b1_row[0:1, :], in_=b1.rearrange("(o h) -> o h", o=1))
+        w2_raw = const.tile([P, PASSES, PACK, G], BF16)
+        nc.sync.dma_start(
+            out=w2_raw[:], in_=w2.rearrange("(g p j) n -> p g j n", p=P, j=PACK)
+        )
+        b2_rows = const.tile([P, P], BF16)
+        for cc in range(G_TILES):
+            nc.scalar.dma_start(
+                out=b2_rows[cc * LINES : (cc + 1) * LINES, :],
+                in_=b2[cc * P : (cc + 1) * P].partition_broadcast(LINES),
+            )
+        for i in range(3, LOAD_AHEAD):
+            load_x(i)
 
         ident = const.tile([P, P], F32)
         make_identity(nc, ident[:])
         eps_col = const.tile([P, 1], F32)
-        nc.vector.memset(eps_col[:], EPS)
+        nc.gpsimd.tensor_scalar(
+            out=eps_col[:], in0=ident[:, 0:1], scalar1=0.0, scalar2=EPS, op0=ALU.mult, op1=ALU.add
+        )
         ones = const.tile([P, P], BF16)
         nc.vector.memset(ones[:], 1.0)
         warm = const.tile([P, 1], F32)
-        nc.scalar.activation(out=warm[:], in_=eps_col[:], func=ACT.Sqrt)
-
-        rows_f32 = const.tile([P, P], F32)
-        nc.vector.tensor_copy(out=rows_f32[:], in_=rows[:])
-        cols_ps = psum.tile([P, P], F32, tag="xT", bufs=1)
-        nc.tensor.transpose(cols_ps[:], rows_f32[:], ident[:])
-        b2_col = const.tile([P, G_TILES], F32)
-        nc.vector.tensor_copy(out=b2_col[:], in_=cols_ps[:, 0:G_TILES])
-        gamma_col = const.tile([P, CHUNKS], F32)
-        nc.vector.tensor_copy(out=gamma_col[:], in_=gamma_raw[:].rearrange("p g j -> p (g j)"))
-        beta_col = const.tile([P, CHUNKS], F32)
-        nc.vector.tensor_copy(out=beta_col[:], in_=beta_raw[:].rearrange("p g j -> p (g j)"))
+        nc.scalar.activation(out=warm[:], in_=ones[:, 0:1], func=ACT.Abs_reciprocal_sqrt)
+        gamma_col = const.tile([P, PASSES * PACK], F32)
+        nc.gpsimd.tensor_copy(out=gamma_col[:], in_=gamma_raw[:].rearrange("p g j -> p (g j)"))
+        beta_col = const.tile([P, PASSES * PACK], F32)
+        nc.gpsimd.tensor_copy(out=beta_col[:], in_=beta_raw[:].rearrange("p g j -> p (g j)"))
 
         b1_all = const.tile([P, H], F32)
         for n in range(HALVES):
@@ -148,193 +139,197 @@ def tile_sub_graph_pb_t_kernel(tc, x_nodes, w1, b1, gamma, beta, w2, b2, out):
                 in_=b1_ps[:].rearrange("p (m j) -> p j m", j=PACK),
             )
 
-        node_max = const.tile([P, G_TILES, TOKENS // NODES], F32)
+        node_max = const.tile([P, G_TILES, LINES], F32)
 
         x_grps = {}
         x_mx = {}
 
-        def transpose_x(blk, i):
-            if not in_range(blk):
+        def transpose_x(i):
+            if not in_range(i):
                 return
-            if i == 0:
-                x_grp = xpool.tile([P, TILES * H], BF16, tag="x_grp", align_bytes=64)
-                x_grps[blk] = x_grp
-            x_words = x_sbs[blk][:].bitcast(F32)
-            x_grp_words = x_grps[blk][:].bitcast(F32)
-            xT_ps = psum.tile([P, PACK, P], F32, tag="xT", bufs=1)
-            for q in range(PACK):
-                g, u = divmod(q, 2)
-                w0 = i * (H // 2) + g * 2 * P
-                nc.tensor.transpose(xT_ps[:, q, :], x_words[:, w0 + u : w0 + 2 * P : 2], ident[:])
+            x_words = x_sbs[i][:].bitcast(F32)
+            xT_ps = psum.tile([P, PASSES, 2, P], F32, tag="xT", bufs=1)
+            for g in range(PASSES):
+                for u in range(2):
+                    w0 = g * 2 * P
+                    nc.tensor.transpose(
+                        xT_ps[:, g, u, :], x_words[:, w0 + u : w0 + 2 * P : 2], ident[:]
+                    )
+            x_grp = xpool.tile([P, H], BF16, tag="x_grp", align_bytes=64)
             nc.scalar.copy(
-                out=x_grp_words[:, i * (H // 2) : (i + 1) * (H // 2)].rearrange(
-                    "p (g w u) -> p g w u", g=PASSES, u=2
-                ),
-                in_=xT_ps[:].rearrange("p (g u) w -> p g w u", g=PASSES),
+                out=x_grp[:].bitcast(F32).rearrange("p (g w u) -> p g w u", g=PASSES, u=2),
+                in_=xT_ps[:].rearrange("p g u w -> p g w u"),
             )
+            x_grps[i] = x_grp
 
-        def quantise_x(blk):
-            if not in_range(blk):
+        def quantise_x(i):
+            if not in_range(i):
                 return
-            x_codes = xpool.tile([P, TILES, PASSES, P], U32, tag="x_codes", align_bytes=64)
-            x_scales = xpool.tile([P, TILES, PASSES, P], U8, tag="x_scales", align_bytes=64)
+            x_codes = xpool.tile([P, PASSES, P], U32, tag="x_codes", align_bytes=64)
+            x_scales = xpool.tile([P, PASSES, P], U8, tag="x_scales", align_bytes=64)
             nc.vector.quantize_mx(
-                out=x_codes[:].rearrange("p i g w -> p (i g w)").bitcast(FP8X4),
-                scales=x_scales[:].rearrange("p i g w -> p (i g w)"),
-                in_=x_grps[blk][:],
+                out=x_codes[:].rearrange("p g w -> p (g w)").bitcast(FP8X4),
+                scales=x_scales[:].rearrange("p g w -> p (g w)"),
+                in_=x_grps[i][:],
             )
-            x_mx[blk] = (x_codes, x_scales)
+            x_mx[i] = (x_codes, x_scales)
 
         h_pss = {}
         h_sbs = {}
         neg_means = {}
         sq_sums = {}
-        stds = {}
 
-        def first_matmul(blk, i, n):
-            if not in_range(blk):
+        def first_matmul(i):
+            if not in_range(i):
                 return
-            x_codes, x_scales = x_mx[blk]
-            cols_n = slice(n * BANK, (n + 1) * BANK)
-            h_ps = psum.tile([P, BANK], F32, tag="h_ps", bufs=4)
-            for g in range(PASSES):
-                nc.tensor.matmul_mx(
-                    out=h_ps[:],
-                    lhsT=x_codes[:, i, g, :].bitcast(FP8X4),
-                    lhsT_scale=x_scales[:, i, g, :],
-                    rhs=w1_codes[:, g, cols_n].bitcast(FP8X4),
-                    rhs_scale=w1_scales[:, g, cols_n],
-                    start=(g == 0),
-                    stop=(g == PASSES - 1),
-                )
-            h_pss[(blk, i, n)] = h_ps
-
-        def add_bias(blk):
-            if not in_range(blk):
-                return
-            h_sb = hpool.tile([P, TILES, H], F32, tag="h_sb")
-            h_sum = stat.tile([P, TILES, HALVES], F32, tag="h_sum")
-            neg_mean = stat.tile([P, TILES], F32, tag="neg_mean")
-            for i in range(TILES):
-                for n in range(HALVES):
-                    cols_n = slice(n * BANK, (n + 1) * BANK)
-                    nc.vector.scalar_tensor_tensor(
-                        out=h_sb[:, i, cols_n].rearrange("p (j m) -> p j m", j=PACK),
-                        in0=h_pss[(blk, i, n)][:].rearrange("p (m j) -> p j m", j=PACK),
-                        scalar=1.0,
-                        in1=b1_all[:, cols_n].rearrange("p (j m) -> p j m", j=PACK),
-                        op0=ALU.mult,
-                        op1=ALU.add,
-                        accum_out=h_sum[:, i, n : n + 1],
+            x_codes, x_scales = x_mx[i]
+            for n in range(HALVES):
+                cols_n = slice(n * BANK, (n + 1) * BANK)
+                h_ps = psum.tile([P, BANK], F32, tag="h_ps", bufs=4)
+                for g in range(PASSES):
+                    nc.tensor.matmul_mx(
+                        out=h_ps[:],
+                        lhsT=x_codes[:, g, :].bitcast(FP8X4),
+                        lhsT_scale=x_scales[:, g, :],
+                        rhs=w1_codes[:, g, cols_n].bitcast(FP8X4),
+                        rhs_scale=w1_scales[:, g, cols_n],
+                        start=(g == 0),
+                        stop=(g == PASSES - 1),
                     )
-                nc.vector.tensor_scalar(
-                    out=neg_mean[:, i : i + 1],
-                    in0=h_sum[:, i, 0:1],
-                    scalar1=h_sum[:, i, 1:2],
-                    scalar2=-1.0 / H,
-                    op0=ALU.add,
-                    op1=ALU.mult,
-                )
-            h_sbs[blk] = h_sb
-            neg_means[blk] = neg_mean
+                h_pss[(i, n)] = h_ps
 
-        def squared_deviations(blk, i):
-            if not in_range(blk):
+        def add_bias(i):
+            if not in_range(i):
                 return
-            if i == 0:
-                sq_sum = stat.tile([P, TILES], F32, tag="sq_sum")
-                sq_sums[blk] = sq_sum
+            h_sb = hpool.tile([P, H], F32, tag="h_sb")
+            h_sum = stat.tile([P, HALVES], F32, tag="h_sum")
+            neg_mean = stat.tile([P, 1], F32, tag="neg_mean")
+            for n in range(HALVES):
+                cols_n = slice(n * BANK, (n + 1) * BANK)
+                nc.vector.scalar_tensor_tensor(
+                    out=h_sb[:, cols_n].rearrange("p (j m) -> p j m", j=PACK),
+                    in0=h_pss[(i, n)][:].rearrange("p (m j) -> p j m", j=PACK),
+                    scalar=1.0,
+                    in1=b1_all[:, cols_n].rearrange("p (j m) -> p j m", j=PACK),
+                    op0=ALU.mult,
+                    op1=ALU.add,
+                    accum_out=h_sum[:, n : n + 1],
+                )
+            nc.vector.tensor_scalar(
+                out=neg_mean[:],
+                in0=h_sum[:, 0:1],
+                scalar1=h_sum[:, 1:2],
+                scalar2=-1.0 / H,
+                op0=ALU.add,
+                op1=ALU.mult,
+            )
+            h_sbs[i] = h_sb
+            neg_means[i] = neg_mean
+
+        def squared_deviations(i):
+            if not in_range(i):
+                return
+            sq_sum = stat.tile([P, 1], F32, tag="sq_sum")
             squares = hpool.tile([P, H], BF16, tag="squares", bufs=2)
             nc.scalar.activation(
                 out=squares[:],
-                in_=h_sbs[blk][:, i, :],
+                in_=h_sbs[i][:],
                 func=ACT.Square,
-                bias=neg_means[blk][:, i : i + 1],
+                bias=neg_means[i][:],
                 scale=1.0,
-                accum_out=sq_sums[blk][:, i : i + 1],
+                accum_out=sq_sum[:],
             )
+            sq_sums[i] = sq_sum
 
-        def standard_deviation(blk):
-            if not in_range(blk):
+        rstds = {}
+
+        def reciprocal_deviation(i):
+            if not in_range(i):
                 return
-            std = stat.tile([P, TILES], F32, tag="std")
+            rstd = stat.tile([P, 1], F32, tag="rstd")
             nc.scalar.activation(
-                out=std[:], in_=sq_sums[blk][:], func=ACT.Sqrt, bias=eps_col[:, 0:1],
-                scale=1.0 / H,
+                out=rstd[:], in_=sq_sums[i][:], func=ACT.Abs_reciprocal_sqrt,
+                bias=eps_col[:], scale=1.0 / H,
             )
-            stds[blk] = std
+            rstds[i] = rstd
 
-        def normalise(blk):
-            if not in_range(blk):
+        def normalise(i):
+            if not in_range(i):
                 return
-            rstd = stat.tile([P, TILES], F32, tag="rstd")
-            nc.vector.reciprocal(out=rstd[:], in_=stds[blk][:])
-            for i in range(TILES):
-                nc.gpsimd.tensor_scalar(
-                    out=h_sbs[blk][:, i, :],
-                    in0=h_sbs[blk][:, i, :],
-                    scalar1=neg_means[blk][:, i : i + 1],
-                    scalar2=rstd[:, i : i + 1],
-                    op0=ALU.add,
-                    op1=ALU.mult,
-                )
+            nc.gpsimd.tensor_scalar(
+                out=h_sbs[i][:],
+                in0=h_sbs[i][:],
+                scalar1=neg_means[i][:],
+                scalar2=rstds[i][:],
+                op0=ALU.add,
+                op1=ALU.mult,
+            )
 
+        nT_pss = {}
         r_planess = {}
         r_grps = {}
         r_mx = {}
 
-        def transpose_and_activate(blk, bank):
-            if not in_range(blk):
+        def transpose_n(i):
+            if not in_range(i):
                 return
-            if bank == 0:
-                r_planes = rpool.tile([P, CHUNKS, BLOCK], BF16, tag="r_planes")
-                r_planess[blk] = r_planes
-            nT_ps = psum.tile([P, CHUNKS_PER_BANK, BLOCK], F32, tag="nT", bufs=2)
-            for s in range(CHUNKS_PER_BANK):
-                c = bank * CHUNKS_PER_BANK + s
-                for i in range(TILES):
-                    nc.tensor.transpose(
-                        nT_ps[:, s, i * P : (i + 1) * P],
-                        h_sbs[blk][:, i, c * P : (c + 1) * P],
-                        ident[:],
-                    )
-            for s in range(CHUNKS_PER_BANK):
-                c = bank * CHUNKS_PER_BANK + s
-                nc.scalar.activation(
-                    out=r_planess[blk][:, c, :],
-                    in_=nT_ps[:, s, :],
-                    func=ACT.Relu,
-                    bias=beta_col[:, c : c + 1],
-                    scale=gamma_col[:, c : c + 1],
-                )
+            for g in range(PASSES):
+                nT_ps = psum.tile([P, PACK, P], F32, tag="nT", bufs=2)
+                for j in range(PACK):
+                    c0 = (PACK * g + j) * P
+                    nc.tensor.transpose(nT_ps[:, j, :], h_sbs[i][:, c0 : c0 + P], ident[:])
+                nT_pss[(i, g)] = nT_ps
 
-        def quantise_r(blk):
-            if not in_range(blk):
+        def activate(i):
+            if not in_range(i):
                 return
-            r_grp = rpool.tile([P, PASSES, BLOCK, PACK], BF16, tag="r_grp", align_bytes=64)
-            r_codes = rpool.tile([P, PASSES, BLOCK], U32, tag="r_codes", align_bytes=64)
-            r_scales = rpool.tile([P, PASSES, BLOCK], U8, tag="r_scales", align_bytes=64)
+            r_planes = rpool.tile([P, PASSES, PACK, P], BF16, tag="r_planes")
             for g in range(PASSES):
-                regroup(nc, r_grp[:, g, :, :], r_planess[blk][:, PACK * g : PACK * (g + 1), :])
+                for j in range(PACK):
+                    c = PACK * g + j
+                    nc.scalar.activation(
+                        out=r_planes[:, g, j, :],
+                        in_=nT_pss[(i, g)][:, j, :],
+                        func=ACT.Relu,
+                        bias=beta_col[:, c : c + 1],
+                        scale=gamma_col[:, c : c + 1],
+                    )
+            r_planess[i] = r_planes
+
+        def regroup_r(i):
+            if not in_range(i):
+                return
+            r_grp = rpool.tile([P, PASSES, P, PACK], BF16, tag="r_grp", align_bytes=64)
             for g in range(PASSES):
-                nc.vector.quantize_mx(
-                    out=r_codes[:, g, :].bitcast(FP8X4),
-                    scales=r_scales[:, g, :],
-                    in_=r_grp[:, g, :, :].rearrange("p w j -> p (w j)"),
-                )
-            r_mx[blk] = (r_codes, r_scales)
+                regroup(nc, r_grp[:, g, :, :], r_planess[i][:, g, :, :])
+            r_grps[i] = r_grp
+
+        def quantise_r(i):
+            if not in_range(i):
+                return
+            r_codes = rpool.tile([P, PASSES, P], U32, tag="r_codes", align_bytes=64)
+            r_scales = rpool.tile([P, PASSES, P], U8, tag="r_scales", align_bytes=64)
+            nc.vector.quantize_mx(
+                out=r_codes[:].rearrange("p g w -> p (g w)").bitcast(FP8X4),
+                scales=r_scales[:].rearrange("p g w -> p (g w)"),
+                in_=r_grps[i][:].rearrange("p g w j -> p (g w j)"),
+            )
+            r_mx[i] = (r_codes, r_scales)
 
         x1_pss = {}
 
-        def second_matmul(blk):
-            if not in_range(blk):
+        def second_matmul(i):
+            if not in_range(i):
                 return
-            r_codes, r_scales = r_mx[blk]
-            x1_ps = psum.tile([P, G_TILES, BLOCK], F32, tag="x1", bufs=1)
+            r_codes, r_scales = r_mx[i]
+            pair, half = divmod(i, PAIR)
+            if half == 0:
+                x1_ps = psum.tile([P, G_TILES, PAIR, P], F32, tag="x1", bufs=1)
+                x1_pss[pair] = x1_ps
             for cc in range(G_TILES):
                 for g in range(PASSES):
                     nc.tensor.matmul_mx(
-                        out=x1_ps[:, cc, :],
+                        out=x1_pss[pair][:, cc, half, :],
                         lhsT=w2_codes[:, g, cc * P : (cc + 1) * P].bitcast(FP8X4),
                         lhsT_scale=w2_scales[:, g, cc * P : (cc + 1) * P],
                         rhs=r_codes[:, g, :].bitcast(FP8X4),
@@ -342,79 +337,89 @@ def tile_sub_graph_pb_t_kernel(tc, x_nodes, w1, b1, gamma, beta, w2, b2, out):
                         start=(g == 0),
                         stop=(g == PASSES - 1),
                     )
-            x1_pss[blk] = x1_ps
 
-        def node_maxima(blk):
-            if not in_range(blk):
+        def node_maxima(i):
+            if not in_range(i) or i % PAIR != PAIR - 1:
                 return
+            pair = i // PAIR
             nc.vector.tensor_reduce(
-                out=node_max[:, :, blk * LINES : (blk + 1) * LINES],
-                in_=x1_pss[blk][:].rearrange("p c (q l) -> p c q l", l=NODES),
+                out=node_max[:, :, pair * PAIR_LINES : (pair + 1) * PAIR_LINES],
+                in_=x1_pss[pair][:].rearrange("p c h (q l) -> p c (h q) l", l=NODES),
                 axis=AX.X,
                 op=ALU.max,
             )
 
-        for blk in range(X_AHEAD):
-            for i in range(TILES):
-                transpose_x(blk, i)
-
         w1_codes = const.tile([P, PASSES, H], U32, align_bytes=64)
         w1_scales = const.tile([P, PASSES, H], U8, align_bytes=64)
-        for g in range(PASSES):
-            w1_grps = {}
-            for n in range(HALVES):
-                w1_grp = wstage.tile([P, BANK, PACK], BF16, tag="w1_grp", align_bytes=64)
-                regroup(nc, w1_grp[:], w1_raws[g][:, :, n * BANK : (n + 1) * BANK])
-                w1_grps[n] = w1_grp
-            for n in range(HALVES):
-                cols_n = slice(n * BANK, (n + 1) * BANK)
-                nc.vector.quantize_mx(
-                    out=w1_codes[:, g, cols_n].bitcast(FP8X4),
-                    scales=w1_scales[:, g, cols_n],
-                    in_=w1_grps[n][:].rearrange("p c t -> p (c t)"),
-                )
-        quantise_x(0)
+        w1_grps = {}
+
+        def regroup_w1(g, n):
+            w1_grp = wstage.tile([P, BANK, PACK], BF16, tag="w1_grp", align_bytes=64)
+            regroup(nc, w1_grp[:], w1_raws[(g, n)][:])
+            w1_grps[(g, n)] = w1_grp
+
+        def quantise_w1(g, n):
+            cols_n = slice(n * BANK, (n + 1) * BANK)
+            nc.vector.quantize_mx(
+                out=w1_codes[:, g, cols_n].bitcast(FP8X4),
+                scales=w1_scales[:, g, cols_n],
+                in_=w1_grps[(g, n)][:].rearrange("p c t -> p (c t)"),
+            )
 
         w2_grp = const.tile([P, PASSES, G, PACK], BF16, align_bytes=64)
         w2_codes = const.tile([P, PASSES, G], U32, align_bytes=64)
         w2_scales = const.tile([P, PASSES, G], U8, align_bytes=64)
-        for g in range(PASSES):
-            regroup(nc, w2_grp[:, g, :, :], w2_raw[:, g, :, :])
-        nc.vector.quantize_mx(
-            out=w2_codes[:].rearrange("p g c -> p (g c)").bitcast(FP8X4),
-            scales=w2_scales[:].rearrange("p g c -> p (g c)"),
-            in_=w2_grp[:].rearrange("p g c t -> p (g c t)"),
-        )
 
-        for step in range(N_BLOCKS + LAG_READ_OUT):
-            load_x(step + LOAD_AHEAD)
-            quantise_x(step + 1)
-            quantise_r(step - LAG_READ_OUT)
-            normalise(step - LAG_NORMALISE)
-            for i in range(TILES):
-                for n in range(HALVES):
-                    first_matmul(step, i, n)
-                squared_deviations(step - LAG_DEVIATION, i)
-                for n in range(HALVES):
-                    transpose_and_activate(step - LAG_TRANSPOSE, i * HALVES + n)
-                transpose_x(step + X_AHEAD, i)
-            second_matmul(step - LAG_READ_OUT)
-            standard_deviation(step - LAG_DEVIATION)
-            add_bias(step)
-            node_maxima(step - LAG_READ_OUT)
+        def regroup_w2():
+            for g in range(PASSES):
+                regroup(nc, w2_grp[:, g, :, :], w2_raw[:, g, :, :])
 
-        for cc in range(G_TILES):
-            nc.vector.tensor_scalar_add(
-                out=node_max[:, cc, :], in0=node_max[:, cc, :], scalar1=b2_col[:, cc : cc + 1]
+        def quantise_w2():
+            nc.vector.quantize_mx(
+                out=w2_codes[:].rearrange("p g c -> p (g c)").bitcast(FP8X4),
+                scales=w2_scales[:].rearrange("p g c -> p (g c)"),
+                in_=w2_grp[:].rearrange("p g c t -> p (g c t)"),
             )
+
+        for i in range(X_AHEAD):
+            transpose_x(i)
+        for n in range(HALVES):
+            for g in range(PASSES):
+                regroup_w1(g, n)
+            if n == 0:
+                quantise_x(0)
+            for g in range(PASSES):
+                quantise_w1(g, n)
+        quantise_x(1)
+        first_matmul(0)
+
+        for i in range(N_TILES + 3):
+            load_x(i + LOAD_AHEAD)
+            normalise(i - 1)
+            first_matmul(i + 1)
+            add_bias(i)
+            node_maxima(i - 3)
+            activate(i - 2)
+            squared_deviations(i)
+            transpose_x(i + X_AHEAD)
+            reciprocal_deviation(i)
+            transpose_n(i - 1)
+            regroup_r(i - 2)
+            quantise_x(i + 2)
+            quantise_r(i - 2)
+            if i == 0:
+                regroup_w2()
+            if i == 1:
+                quantise_w2()
+            second_matmul(i - 2)
+
         maxT_ps = psum.tile([P, P], F32, tag="xT", bufs=1)
         nc.tensor.transpose(maxT_ps[:], node_max[:].rearrange("p c b -> p (c b)"), ident[:])
         result = const.tile([P, 2, P], F32)
         for rep in range(2):
-            nc.vector.tensor_copy(out=result[:, rep, :], in_=maxT_ps[:])
-        out_view = out.rearrange("b (r c j) -> c b r j", r=2, c=G_TILES)
-        n_lines = TOKENS // NODES
-        for cc in range(G_TILES):
-            nc.sync.dma_start(
-                out=out_view[cc], in_=result[cc * n_lines : (cc + 1) * n_lines, :, :]
+            nc.vector.tensor_tensor(
+                out=result[:, rep, :], in0=maxT_ps[:], in1=b2_rows[:], op=ALU.add
             )
+        out_view = out.rearrange("b (r c j) -> c b r j", r=2, c=G_TILES)
+        for cc in range(G_TILES):
+            nc.sync.dma_start(out=out_view[cc], in_=result[cc * LINES : (cc + 1) * LINES, :, :])

@@ -28,6 +28,7 @@ N_TILES = TOKENS // P
 HALVES = H // BANK
 G_TILES = G // P
 PAIR = 2
+N_PAIRS = N_TILES // PAIR
 PAIR_LINES = PAIR * P // NODES
 
 X_AHEAD = 3
@@ -51,8 +52,8 @@ def tile_sub_graph_pb_t_kernel(tc, x_nodes, w1, b1, gamma, beta, w2, b2, out):
         const = ctx.enter_context(tc.tile_pool(name="const", bufs=1))
         wstage = ctx.enter_context(tc.tile_pool(name="wstage", bufs=2))
         xpool = ctx.enter_context(tc.tile_pool(name="xpool", bufs=3))
-        hpool = ctx.enter_context(tc.tile_pool(name="hpool", bufs=4))
-        stat = ctx.enter_context(tc.tile_pool(name="stat", bufs=4))
+        hpool = ctx.enter_context(tc.tile_pool(name="hpool", bufs=6))
+        stat = ctx.enter_context(tc.tile_pool(name="stat", bufs=6))
         rpool = ctx.enter_context(tc.tile_pool(name="rpool", bufs=2))
         psum = ctx.enter_context(tc.psum_pool(name="psum", bufs=1))
         ctx.enter_context(tc.manual_schedule())
@@ -176,6 +177,7 @@ def tile_sub_graph_pb_t_kernel(tc, x_nodes, w1, b1, gamma, beta, w2, b2, out):
 
         h_pss = {}
         h_sbs = {}
+        h_sums = {}
         neg_means = {}
         sq_sums = {}
 
@@ -203,7 +205,6 @@ def tile_sub_graph_pb_t_kernel(tc, x_nodes, w1, b1, gamma, beta, w2, b2, out):
                 return
             h_sb = hpool.tile([P, H], F32, tag="h_sb")
             h_sum = stat.tile([P, HALVES], F32, tag="h_sum")
-            neg_mean = stat.tile([P, 1], F32, tag="neg_mean")
             for n in range(HALVES):
                 cols_n = slice(n * BANK, (n + 1) * BANK)
                 nc.vector.scalar_tensor_tensor(
@@ -215,15 +216,21 @@ def tile_sub_graph_pb_t_kernel(tc, x_nodes, w1, b1, gamma, beta, w2, b2, out):
                     op1=ALU.add,
                     accum_out=h_sum[:, n : n + 1],
                 )
+            h_sbs[i] = h_sb
+            h_sums[i] = h_sum
+
+        def negative_mean(i):
+            if not in_range(i):
+                return
+            neg_mean = stat.tile([P, 1], F32, tag="neg_mean")
             nc.vector.tensor_scalar(
                 out=neg_mean[:],
-                in0=h_sum[:, 0:1],
-                scalar1=h_sum[:, 1:2],
+                in0=h_sums[i][:, 0:1],
+                scalar1=h_sums[i][:, 1:2],
                 scalar2=-1.0 / H,
                 op0=ALU.add,
                 op1=ALU.mult,
             )
-            h_sbs[i] = h_sb
             neg_means[i] = neg_mean
 
         def squared_deviations(i):
@@ -270,66 +277,80 @@ def tile_sub_graph_pb_t_kernel(tc, x_nodes, w1, b1, gamma, beta, w2, b2, out):
         r_grps = {}
         r_mx = {}
 
-        def transpose_n(i):
-            if not in_range(i):
-                return
-            for g in range(PASSES):
-                nT_ps = psum.tile([P, PACK, P], F32, tag="nT", bufs=2)
-                for j in range(PACK):
-                    c0 = (PACK * g + j) * P
-                    nc.tensor.transpose(nT_ps[:, j, :], h_sbs[i][:, c0 : c0 + P], ident[:])
-                nT_pss[(i, g)] = nT_ps
 
-        def activate(i):
-            if not in_range(i):
-                return
-            r_planes = rpool.tile([P, PASSES, PACK, P], BF16, tag="r_planes")
-            for g in range(PASSES):
-                for j in range(PACK):
-                    c = PACK * g + j
-                    nc.scalar.activation(
-                        out=r_planes[:, g, j, :],
-                        in_=nT_pss[(i, g)][:, j, :],
-                        func=ACT.Relu,
-                        bias=beta_col[:, c : c + 1],
-                        scale=gamma_col[:, c : c + 1],
-                    )
-            r_planess[i] = r_planes
+        def unit(u):
+            return divmod(u, PASSES)
 
-        def regroup_r(i):
-            if not in_range(i):
-                return
-            r_grp = rpool.tile([P, PASSES, P, PACK], BF16, tag="r_grp", align_bytes=64)
-            for g in range(PASSES):
-                regroup(nc, r_grp[:, g, :, :], r_planess[i][:, g, :, :])
-            r_grps[i] = r_grp
+        def unit_in_range(u):
+            return 0 <= u < N_PAIRS * PASSES
 
-        def quantise_r(i):
-            if not in_range(i):
+        def transpose_n(u):
+            if not unit_in_range(u):
                 return
-            r_codes = rpool.tile([P, PASSES, P], U32, tag="r_codes", align_bytes=64)
-            r_scales = rpool.tile([P, PASSES, P], U8, tag="r_scales", align_bytes=64)
+            pair, g = unit(u)
+            for b in range(PACK // 2):
+                nT_ps = psum.tile([P, 2, PAIR * P], F32, tag="nT", bufs=2)
+                for s in range(2):
+                    c0 = (PACK * g + 2 * b + s) * P
+                    for half in range(PAIR):
+                        nc.tensor.transpose(
+                            nT_ps[:, s, half * P : (half + 1) * P],
+                            h_sbs[PAIR * pair + half][:, c0 : c0 + P],
+                            ident[:],
+                        )
+                nT_pss[(u, b)] = nT_ps
+
+        def activate(u):
+            if not unit_in_range(u):
+                return
+            pair, g = unit(u)
+            r_planes = rpool.tile([P, PACK, PAIR * P], BF16, tag="r_planes")
+            r_planess[u] = r_planes
+            for j in range(PACK):
+                c = PACK * g + j
+                nc.scalar.activation(
+                    out=r_planess[u][:, j, :],
+                    in_=nT_pss[(u, j // 2)][:, j % 2, :],
+                    func=ACT.Relu,
+                    bias=beta_col[:, c : c + 1],
+                    scale=gamma_col[:, c : c + 1],
+                )
+
+        def regroup_r(u):
+            if not unit_in_range(u):
+                return
+            r_grp = rpool.tile([P, PAIR * P, PACK], BF16, tag="r_grp", align_bytes=64)
+            regroup(nc, r_grp[:], r_planess[u][:])
+            r_grps[u] = r_grp
+
+        def quantise_r(u):
+            if not unit_in_range(u):
+                return
+            pair, g = unit(u)
+            if g == 0:
+                r_codes = rpool.tile([P, PASSES, PAIR * P], U32, tag="r_codes", align_bytes=64)
+                r_scales = rpool.tile([P, PASSES, PAIR * P], U8, tag="r_scales", align_bytes=64)
+                r_mx[pair] = (r_codes, r_scales)
+            r_codes, r_scales = r_mx[pair]
             nc.vector.quantize_mx(
-                out=r_codes[:].rearrange("p g w -> p (g w)").bitcast(FP8X4),
-                scales=r_scales[:].rearrange("p g w -> p (g w)"),
-                in_=r_grps[i][:].rearrange("p g w j -> p (g w j)"),
+                out=r_codes[:, g, :].bitcast(FP8X4),
+                scales=r_scales[:, g, :],
+                in_=r_grps[u][:].rearrange("p w j -> p (w j)"),
             )
-            r_mx[i] = (r_codes, r_scales)
 
         x1_pss = {}
 
-        def second_matmul(i):
-            if not in_range(i):
+        def second_matmul(u):
+            if not unit_in_range(u) or unit(u)[1] != PASSES - 1:
                 return
-            r_codes, r_scales = r_mx[i]
-            pair, half = divmod(i, PAIR)
-            if half == 0:
-                x1_ps = psum.tile([P, G_TILES, PAIR, P], F32, tag="x1", bufs=1)
-                x1_pss[pair] = x1_ps
+            pair = unit(u)[0]
+            r_codes, r_scales = r_mx[pair]
+            x1_ps = psum.tile([P, G_TILES, PAIR * P], F32, tag="x1", bufs=1)
+            x1_pss[pair] = x1_ps
             for cc in range(G_TILES):
                 for g in range(PASSES):
                     nc.tensor.matmul_mx(
-                        out=x1_pss[pair][:, cc, half, :],
+                        out=x1_ps[:, cc, :],
                         lhsT=w2_codes[:, g, cc * P : (cc + 1) * P].bitcast(FP8X4),
                         lhsT_scale=w2_scales[:, g, cc * P : (cc + 1) * P],
                         rhs=r_codes[:, g, :].bitcast(FP8X4),
@@ -338,13 +359,13 @@ def tile_sub_graph_pb_t_kernel(tc, x_nodes, w1, b1, gamma, beta, w2, b2, out):
                         stop=(g == PASSES - 1),
                     )
 
-        def node_maxima(i):
-            if not in_range(i) or i % PAIR != PAIR - 1:
+        def node_maxima(u):
+            if not unit_in_range(u):
                 return
-            pair = i // PAIR
+            pair, cc = divmod(u, G_TILES)
             nc.vector.tensor_reduce(
-                out=node_max[:, :, pair * PAIR_LINES : (pair + 1) * PAIR_LINES],
-                in_=x1_pss[pair][:].rearrange("p c h (q l) -> p c (h q) l", l=NODES),
+                out=node_max[:, cc, pair * PAIR_LINES : (pair + 1) * PAIR_LINES],
+                in_=x1_pss[pair][:, cc, :].rearrange("p (q l) -> p q l", l=NODES),
                 axis=AX.X,
                 op=ALU.max,
             )
@@ -393,25 +414,26 @@ def tile_sub_graph_pb_t_kernel(tc, x_nodes, w1, b1, gamma, beta, w2, b2, out):
         quantise_x(1)
         first_matmul(0)
 
-        for i in range(N_TILES + 3):
+        for i in range(N_TILES + 5):
             load_x(i + LOAD_AHEAD)
             normalise(i - 1)
-            first_matmul(i + 1)
             add_bias(i)
-            node_maxima(i - 3)
-            activate(i - 2)
+            node_maxima(i - 5)
+            negative_mean(i)
+            activate(i - 3)
             squared_deviations(i)
+            first_matmul(i + 1)
             transpose_x(i + X_AHEAD)
             reciprocal_deviation(i)
-            transpose_n(i - 1)
-            regroup_r(i - 2)
+            transpose_n(i - 2)
+            regroup_r(i - 3)
             quantise_x(i + 2)
-            quantise_r(i - 2)
+            quantise_r(i - 3)
             if i == 0:
                 regroup_w2()
             if i == 1:
                 quantise_w2()
-            second_matmul(i - 2)
+            second_matmul(i - 3)
 
         maxT_ps = psum.tile([P, P], F32, tag="xT", bufs=1)
         nc.tensor.transpose(maxT_ps[:], node_max[:].rearrange("p c b -> p (c b)"), ident[:])

@@ -29,16 +29,18 @@ HALVES = H // BANK
 G_TILES = G // P
 PAIR = 2
 N_PAIRS = N_TILES // PAIR
-PAIR_LINES = PAIR * P // NODES
+N_UNITS = N_TILES
+SHARED_UNIT = N_UNITS - 4
 
+VECTOR_COLS = 352
 X_AHEAD = 3
 LOAD_AHEAD = 8
 
 FLOPS = 2 * TOKENS * H * H + 2 * TOKENS * H * G
 
 
-def regroup(nc, grouped, planes):
-    nc.vector.tensor_copy(
+def regroup(copy, grouped, planes):
+    copy(
         out=grouped.rearrange("p (c i) t -> p c t i", i=4),
         in_=planes.rearrange("p t (c i) -> p c t i", i=4),
     )
@@ -50,7 +52,7 @@ def tile_sub_graph_pb_t_kernel(tc, x_nodes, w1, b1, gamma, beta, w2, b2, out):
 
     with ExitStack() as ctx:
         const = ctx.enter_context(tc.tile_pool(name="const", bufs=1))
-        wstage = ctx.enter_context(tc.tile_pool(name="wstage", bufs=2))
+        wstage = ctx.enter_context(tc.tile_pool(name="wstage", bufs=4))
         xpool = ctx.enter_context(tc.tile_pool(name="xpool", bufs=3))
         hpool = ctx.enter_context(tc.tile_pool(name="hpool", bufs=6))
         stat = ctx.enter_context(tc.tile_pool(name="stat", bufs=6))
@@ -82,15 +84,18 @@ def tile_sub_graph_pb_t_kernel(tc, x_nodes, w1, b1, gamma, beta, w2, b2, out):
             )
             w1_raws[(g, n)] = w1_raw
 
+        warm = const.tile([P, 1], F32)
+        nc.vector.memset(warm[:], 1.0)
+        nc.scalar.activation(out=warm[:], in_=warm[:], func=ACT.Abs_reciprocal_sqrt)
         b1_row = const.tile([P, H], BF16)
         nc.vector.memset(b1_row[:], 0.0)
-        load_w1(0, 0)
         load_x(0)
+        load_w1(0, 0)
         load_w1(1, 0)
         load_x(1)
         load_w1(0, 1)
-        load_x(2)
         load_w1(1, 1)
+        load_x(2)
         nc.scalar.dma_start(out=b1_row[0:1, :], in_=b1.rearrange("(o h) -> o h", o=1))
         gamma_raw = const.tile([P, PASSES, PACK], BF16)
         nc.scalar.dma_start(
@@ -121,22 +126,21 @@ def tile_sub_graph_pb_t_kernel(tc, x_nodes, w1, b1, gamma, beta, w2, b2, out):
         )
         ones = const.tile([P, P], BF16)
         nc.vector.memset(ones[:], 1.0)
-        warm = const.tile([P, 1], F32)
-        nc.scalar.activation(out=warm[:], in_=ones[:, 0:1], func=ACT.Abs_reciprocal_sqrt)
         gamma_col = const.tile([P, PASSES * PACK], F32)
         nc.gpsimd.tensor_copy(out=gamma_col[:], in_=gamma_raw[:].rearrange("p g j -> p (g j)"))
         beta_col = const.tile([P, PASSES * PACK], F32)
         nc.gpsimd.tensor_copy(out=beta_col[:], in_=beta_raw[:].rearrange("p g j -> p (g j)"))
 
         b1_all = const.tile([P, H], F32)
-        for n in range(HALVES):
+
+        def spread_b1(n):
+            cols_n = slice(n * BANK, (n + 1) * BANK)
             b1_ps = psum.tile([P, BANK], F32, tag="h_ps", bufs=4)
             nc.tensor.matmul(
-                out=b1_ps[:], lhsT=ones[:], rhs=b1_row[:, n * BANK : (n + 1) * BANK],
-                start=True, stop=True,
+                out=b1_ps[:], lhsT=ones[:], rhs=b1_row[:, cols_n], start=True, stop=True
             )
             nc.scalar.copy(
-                out=b1_all[:, n * BANK : (n + 1) * BANK].rearrange("p (j m) -> p j m", j=PACK),
+                out=b1_all[:, cols_n].rearrange("p (j m) -> p j m", j=PACK),
                 in_=b1_ps[:].rearrange("p (m j) -> p j m", j=PACK),
             )
 
@@ -181,11 +185,11 @@ def tile_sub_graph_pb_t_kernel(tc, x_nodes, w1, b1, gamma, beta, w2, b2, out):
         neg_means = {}
         sq_sums = {}
 
-        def first_matmul(i):
+        def first_matmul(i, halves=range(HALVES)):
             if not in_range(i):
                 return
             x_codes, x_scales = x_mx[i]
-            for n in range(HALVES):
+            for n in halves:
                 cols_n = slice(n * BANK, (n + 1) * BANK)
                 h_ps = psum.tile([P, BANK], F32, tag="h_ps", bufs=4)
                 for g in range(PASSES):
@@ -263,7 +267,8 @@ def tile_sub_graph_pb_t_kernel(tc, x_nodes, w1, b1, gamma, beta, w2, b2, out):
         def normalise(i):
             if not in_range(i):
                 return
-            nc.gpsimd.tensor_scalar(
+            engine = nc.vector if i == N_TILES - 1 else nc.gpsimd
+            engine.tensor_scalar(
                 out=h_sbs[i][:],
                 in0=h_sbs[i][:],
                 scalar1=neg_means[i][:],
@@ -278,97 +283,162 @@ def tile_sub_graph_pb_t_kernel(tc, x_nodes, w1, b1, gamma, beta, w2, b2, out):
         r_mx = {}
 
 
-        def unit(u):
-            return divmod(u, PASSES)
-
         def unit_in_range(u):
-            return 0 <= u < N_PAIRS * PASSES
+            return 0 <= u < N_UNITS
+
+        def single(u):
+            return u // PAIR == N_PAIRS - 1
+
+        def unit_tiles(u):
+            pair, part = divmod(u, PAIR)
+            return [PAIR * pair + part] if single(u) else [PAIR * pair, PAIR * pair + 1]
+
+        def unit_passes(u):
+            return range(PASSES) if single(u) else [u % PASSES]
+
+        def unit_chunks(u):
+            return [PACK * g + j for g in unit_passes(u) for j in range(PACK)]
+
+        def unit_width(u):
+            return P * len(unit_tiles(u))
 
         def transpose_n(u):
             if not unit_in_range(u):
                 return
-            pair, g = unit(u)
-            for b in range(PACK // 2):
-                nT_ps = psum.tile([P, 2, PAIR * P], F32, tag="nT", bufs=2)
-                for s in range(2):
-                    c0 = (PACK * g + 2 * b + s) * P
-                    for half in range(PAIR):
-                        nc.tensor.transpose(
-                            nT_ps[:, s, half * P : (half + 1) * P],
-                            h_sbs[PAIR * pair + half][:, c0 : c0 + P],
-                            ident[:],
-                        )
-                nT_pss[(u, b)] = nT_ps
+            width = unit_width(u)
+            per_bank = BANK // width
+            for q, c in enumerate(unit_chunks(u)):
+                if q % per_bank == 0:
+                    tag, bufs = ("h_ps", 4) if single(u) else ("nT", 2)
+                    nT_ps = psum.tile([P, BANK], F32, tag=tag, bufs=bufs)
+                for part, i in enumerate(unit_tiles(u)):
+                    col = (q % per_bank) * width + part * P
+                    nc.tensor.transpose(
+                        nT_ps[:, col : col + P], h_sbs[i][:, c * P : (c + 1) * P], ident[:]
+                    )
+                nT_pss[(u, q)] = nT_ps[:, (q % per_bank) * width : (q % per_bank + 1) * width]
 
-        def activate(u):
+        def activate(u, first):
             if not unit_in_range(u):
                 return
-            pair, g = unit(u)
-            r_planes = rpool.tile([P, PACK, PAIR * P], BF16, tag="r_planes")
-            r_planess[u] = r_planes
-            for j in range(PACK):
-                c = PACK * g + j
-                nc.scalar.activation(
-                    out=r_planess[u][:, j, :],
-                    in_=nT_pss[(u, j // 2)][:, j % 2, :],
-                    func=ACT.Relu,
-                    bias=beta_col[:, c : c + 1],
-                    scale=gamma_col[:, c : c + 1],
-                )
+            width = unit_width(u)
+            chunks = unit_chunks(u)
+            if first:
+                r_planes = rpool.tile([P, PACK * PAIR * P], BF16, tag="r_planes", bufs=3)
+                r_planess[u] = r_planes
+            for q, c in enumerate(chunks):
+                if (q == 0) != first:
+                    continue
+                plane = r_planess[u][:, q * width : (q + 1) * width]
+                if u == SHARED_UNIT and q >= len(chunks) // 2:
+                    nc.vector.tensor_scalar(
+                        out=plane,
+                        in0=nT_pss[(u, q)],
+                        scalar1=gamma_col[:, c : c + 1],
+                        scalar2=beta_col[:, c : c + 1],
+                        op0=ALU.mult,
+                        op1=ALU.add,
+                    )
+                else:
+                    nc.scalar.activation(
+                        out=plane,
+                        in_=nT_pss[(u, q)],
+                        func=ACT.Relu,
+                        bias=beta_col[:, c : c + 1],
+                        scale=gamma_col[:, c : c + 1],
+                    )
+
+        def relu_copy(out, in_):
+            nc.vector.tensor_scalar_max(out=out, in0=in_, scalar1=0.0)
 
         def regroup_r(u):
             if not unit_in_range(u):
                 return
-            r_grp = rpool.tile([P, PAIR * P, PACK], BF16, tag="r_grp", align_bytes=64)
-            regroup(nc, r_grp[:], r_planess[u][:])
+            r_grp = rpool.tile([P, PACK * PAIR * P], BF16, tag="r_grp", align_bytes=64)
+            size = PACK * unit_width(u)
+            copy = relu_copy if u == SHARED_UNIT else nc.vector.tensor_copy
+            for k in range(len(unit_passes(u))):
+                part = slice(k * size, (k + 1) * size)
+                regroup(
+                    copy,
+                    r_grp[:, part].rearrange("p (w j) -> p w j", j=PACK),
+                    r_planess[u][:, part].rearrange("p (j w) -> p j w", j=PACK),
+                )
             r_grps[u] = r_grp
 
         def quantise_r(u):
             if not unit_in_range(u):
                 return
-            pair, g = unit(u)
-            if g == 0:
-                r_codes = rpool.tile([P, PASSES, PAIR * P], U32, tag="r_codes", align_bytes=64)
-                r_scales = rpool.tile([P, PASSES, PAIR * P], U8, tag="r_scales", align_bytes=64)
-                r_mx[pair] = (r_codes, r_scales)
-            r_codes, r_scales = r_mx[pair]
+            words = PAIR * P
+            if single(u) or u % PASSES == 0:
+                r_codes = rpool.tile([P, PASSES * words], U32, tag="r_codes", align_bytes=64)
+                r_scales = rpool.tile([P, PASSES * words], U8, tag="r_scales", align_bytes=64)
+                r_mx[u] = (r_codes, r_scales)
+                cols = slice(0, words)
+            else:
+                r_mx[u] = r_mx[u - 1]
+                cols = slice(words, 2 * words)
+            r_codes, r_scales = r_mx[u]
             nc.vector.quantize_mx(
-                out=r_codes[:, g, :].bitcast(FP8X4),
-                scales=r_scales[:, g, :],
-                in_=r_grps[u][:].rearrange("p w j -> p (w j)"),
+                out=r_codes[:, cols].bitcast(FP8X4),
+                scales=r_scales[:, cols],
+                in_=r_grps[u][:],
             )
 
         x1_pss = {}
 
+        def x1_work(u):
+            if not unit_in_range(u):
+                return None
+            pair, part = divmod(u, PAIR)
+            if single(u):
+                return ("tile", u), range(G_TILES), unit_tiles(u)
+            if part == 1:
+                chunks = [0] if pair < N_PAIRS - 2 else range(G_TILES)
+                return ("pair", pair), chunks, unit_tiles(u)
+            if pair > 0:
+                return ("pair", pair - 1), [1], unit_tiles(u - 1)
+            return None
+
         def second_matmul(u):
-            if not unit_in_range(u) or unit(u)[1] != PASSES - 1:
+            work = x1_work(u)
+            if work is None:
                 return
-            pair = unit(u)[0]
-            r_codes, r_scales = r_mx[pair]
-            x1_ps = psum.tile([P, G_TILES, PAIR * P], F32, tag="x1", bufs=1)
-            x1_pss[pair] = x1_ps
-            for cc in range(G_TILES):
+            key, chunks, tiles = work
+            if key not in x1_pss:
+                tag, bufs = ("x1", 1) if len(tiles) == PAIR else ("nT", 2)
+                x1_ps = psum.tile([P, G_TILES, PAIR * P], F32, tag=tag, bufs=bufs)
+                x1_pss[key] = x1_ps
+            r_codes, r_scales = r_mx[tiles[-1]]
+            width = P * len(tiles)
+            for cc in chunks:
                 for g in range(PASSES):
+                    words = slice(g * width, (g + 1) * width)
                     nc.tensor.matmul_mx(
-                        out=x1_ps[:, cc, :],
+                        out=x1_pss[key][:, cc, 0:width],
                         lhsT=w2_codes[:, g, cc * P : (cc + 1) * P].bitcast(FP8X4),
                         lhsT_scale=w2_scales[:, g, cc * P : (cc + 1) * P],
-                        rhs=r_codes[:, g, :].bitcast(FP8X4),
-                        rhs_scale=r_scales[:, g, :],
+                        rhs=r_codes[:, words].bitcast(FP8X4),
+                        rhs_scale=r_scales[:, words],
                         start=(g == 0),
                         stop=(g == PASSES - 1),
                     )
 
         def node_maxima(u):
-            if not unit_in_range(u):
+            work = x1_work(u)
+            if work is None:
                 return
-            pair, cc = divmod(u, G_TILES)
-            nc.vector.tensor_reduce(
-                out=node_max[:, cc, pair * PAIR_LINES : (pair + 1) * PAIR_LINES],
-                in_=x1_pss[pair][:, cc, :].rearrange("p (q l) -> p q l", l=NODES),
-                axis=AX.X,
-                op=ALU.max,
-            )
+            key, chunks, tiles = work
+            lines = P // NODES
+            for cc in chunks:
+                nc.vector.tensor_reduce(
+                    out=node_max[:, cc, lines * tiles[0] : lines * (tiles[-1] + 1)],
+                    in_=x1_pss[key][:, cc, 0 : P * len(tiles)].rearrange(
+                        "p (q l) -> p q l", l=NODES
+                    ),
+                    axis=AX.X,
+                    op=ALU.max,
+                )
 
         w1_codes = const.tile([P, PASSES, H], U32, align_bytes=64)
         w1_scales = const.tile([P, PASSES, H], U8, align_bytes=64)
@@ -376,7 +446,10 @@ def tile_sub_graph_pb_t_kernel(tc, x_nodes, w1, b1, gamma, beta, w2, b2, out):
 
         def regroup_w1(g, n):
             w1_grp = wstage.tile([P, BANK, PACK], BF16, tag="w1_grp", align_bytes=64)
-            regroup(nc, w1_grp[:], w1_raws[(g, n)][:])
+            w1_raw = w1_raws[(g, n)]
+            mid = VECTOR_COLS
+            regroup(nc.vector.tensor_copy, w1_grp[:, :mid, :], w1_raw[:, :, :mid])
+            regroup(nc.scalar.copy, w1_grp[:, mid:, :], w1_raw[:, :, mid:])
             w1_grps[(g, n)] = w1_grp
 
         def quantise_w1(g, n):
@@ -393,7 +466,7 @@ def tile_sub_graph_pb_t_kernel(tc, x_nodes, w1, b1, gamma, beta, w2, b2, out):
 
         def regroup_w2():
             for g in range(PASSES):
-                regroup(nc, w2_grp[:, g, :, :], w2_raw[:, g, :, :])
+                regroup(nc.vector.tensor_copy, w2_grp[:, g, :, :], w2_raw[:, g, :, :])
 
         def quantise_w2():
             nc.vector.quantize_mx(
@@ -402,46 +475,51 @@ def tile_sub_graph_pb_t_kernel(tc, x_nodes, w1, b1, gamma, beta, w2, b2, out):
                 in_=w2_grp[:].rearrange("p g c t -> p (g c t)"),
             )
 
-        for i in range(X_AHEAD):
-            transpose_x(i)
-        for n in range(HALVES):
-            for g in range(PASSES):
-                regroup_w1(g, n)
-            if n == 0:
-                quantise_x(0)
-            for g in range(PASSES):
-                quantise_w1(g, n)
+        transpose_x(0)
+        regroup_w1(0, 0)
+        regroup_w1(1, 0)
+        spread_b1(0)
+        transpose_x(1)
+        quantise_w1(0, 0)
+        quantise_x(0)
+        quantise_w1(1, 0)
+        first_matmul(0, (0,))
+        regroup_w1(0, 1)
+        regroup_w1(1, 1)
+        spread_b1(1)
+        quantise_w1(0, 1)
         quantise_x(1)
-        first_matmul(0)
+        quantise_w1(1, 1)
+        first_matmul(0, (1,))
+        transpose_x(2)
 
-        for i in range(N_TILES + 5):
+        for i in range(N_TILES + 6):
             load_x(i + LOAD_AHEAD)
             normalise(i - 1)
             add_bias(i)
-            node_maxima(i - 5)
+            node_maxima(i - 6)
             negative_mean(i)
-            activate(i - 3)
             squared_deviations(i)
-            first_matmul(i + 1)
-            transpose_x(i + X_AHEAD)
+            activate(i - 3, first=True)
             reciprocal_deviation(i)
+            activate(i - 3, first=False)
+            first_matmul(i + 1)
+            second_matmul(i - 5)
+            transpose_x(i + X_AHEAD)
             transpose_n(i - 2)
-            regroup_r(i - 3)
+            regroup_r(i - 4)
             quantise_x(i + 2)
-            quantise_r(i - 3)
+            quantise_r(i - 4)
             if i == 0:
                 regroup_w2()
             if i == 1:
                 quantise_w2()
-            second_matmul(i - 3)
 
         maxT_ps = psum.tile([P, P], F32, tag="xT", bufs=1)
         nc.tensor.transpose(maxT_ps[:], node_max[:].rearrange("p c b -> p (c b)"), ident[:])
-        result = const.tile([P, 2, P], F32)
-        for rep in range(2):
-            nc.vector.tensor_tensor(
-                out=result[:, rep, :], in0=maxT_ps[:], in1=b2_rows[:], op=ALU.add
-            )
-        out_view = out.rearrange("b (r c j) -> c b r j", r=2, c=G_TILES)
-        for cc in range(G_TILES):
-            nc.sync.dma_start(out=out_view[cc], in_=result[cc * LINES : (cc + 1) * LINES, :, :])
+        result = const.tile([P, P], F32)
+        nc.vector.tensor_tensor(out=result[:], in0=maxT_ps[:], in1=b2_rows[:], op=ALU.add)
+        out_view = out.rearrange("b (r c j) -> r c b j", r=2, c=G_TILES)
+        for r, queue in enumerate((nc.sync, nc.scalar)):
+            for cc in range(G_TILES):
+                queue.dma_start(out=out_view[r, cc], in_=result[cc * LINES : (cc + 1) * LINES, :])

@@ -30,7 +30,7 @@ G_TILES = G // P
 PAIR = 2
 N_PAIRS = N_TILES // PAIR
 N_UNITS = N_TILES
-SHARED_UNIT = N_UNITS - 4
+VECTOR_TILES = 2
 
 VECTOR_COLS = 352
 X_AHEAD = 3
@@ -86,7 +86,7 @@ def tile_sub_graph_pb_t_kernel(tc, x_nodes, w1, b1, gamma, beta, w2, b2, out):
 
         warm = const.tile([P, 1], F32)
         nc.vector.memset(warm[:], 1.0)
-        nc.scalar.activation(out=warm[:], in_=warm[:], func=ACT.Abs_reciprocal_sqrt)
+        nc.scalar.activation(out=warm[:], in_=warm[:], func=ACT.Sqrt)
         b1_row = const.tile([P, H], BF16)
         nc.vector.memset(b1_row[:], 0.0)
         load_x(0)
@@ -252,22 +252,28 @@ def tile_sub_graph_pb_t_kernel(tc, x_nodes, w1, b1, gamma, beta, w2, b2, out):
             )
             sq_sums[i] = sq_sum
 
+        stds = {}
         rstds = {}
+
+        def standard_deviation(i):
+            if not in_range(i):
+                return
+            std = stat.tile([P, 1], F32, tag="std")
+            nc.scalar.activation(
+                out=std[:], in_=sq_sums[i][:], func=ACT.Sqrt, bias=eps_col[:], scale=1.0 / H
+            )
+            stds[i] = std
 
         def reciprocal_deviation(i):
             if not in_range(i):
                 return
             rstd = stat.tile([P, 1], F32, tag="rstd")
-            nc.scalar.activation(
-                out=rstd[:], in_=sq_sums[i][:], func=ACT.Abs_reciprocal_sqrt,
-                bias=eps_col[:], scale=1.0 / H,
-            )
+            nc.vector.reciprocal(out=rstd[:], in_=stds[i][:])
             rstds[i] = rstd
 
-        def normalise(i):
+        def normalise(engine, i):
             if not in_range(i):
                 return
-            engine = nc.vector if i == N_TILES - 1 else nc.gpsimd
             engine.tensor_scalar(
                 out=h_sbs[i][:],
                 in0=h_sbs[i][:],
@@ -322,45 +328,28 @@ def tile_sub_graph_pb_t_kernel(tc, x_nodes, w1, b1, gamma, beta, w2, b2, out):
             if not unit_in_range(u):
                 return
             width = unit_width(u)
-            chunks = unit_chunks(u)
             if first:
                 r_planes = rpool.tile([P, PACK * PAIR * P], BF16, tag="r_planes", bufs=3)
                 r_planess[u] = r_planes
-            for q, c in enumerate(chunks):
-                if (q == 0) != first:
-                    continue
-                plane = r_planess[u][:, q * width : (q + 1) * width]
-                if u == SHARED_UNIT and q >= len(chunks) // 2:
-                    nc.vector.tensor_scalar(
-                        out=plane,
-                        in0=nT_pss[(u, q)],
-                        scalar1=gamma_col[:, c : c + 1],
-                        scalar2=beta_col[:, c : c + 1],
-                        op0=ALU.mult,
-                        op1=ALU.add,
-                    )
-                else:
+            for q, c in enumerate(unit_chunks(u)):
+                if (q == 0) == first:
                     nc.scalar.activation(
-                        out=plane,
+                        out=r_planess[u][:, q * width : (q + 1) * width],
                         in_=nT_pss[(u, q)],
                         func=ACT.Relu,
                         bias=beta_col[:, c : c + 1],
                         scale=gamma_col[:, c : c + 1],
                     )
 
-        def relu_copy(out, in_):
-            nc.vector.tensor_scalar_max(out=out, in0=in_, scalar1=0.0)
-
         def regroup_r(u):
             if not unit_in_range(u):
                 return
             r_grp = rpool.tile([P, PACK * PAIR * P], BF16, tag="r_grp", align_bytes=64)
             size = PACK * unit_width(u)
-            copy = relu_copy if u == SHARED_UNIT else nc.vector.tensor_copy
             for k in range(len(unit_passes(u))):
                 part = slice(k * size, (k + 1) * size)
                 regroup(
-                    copy,
+                    nc.vector.tensor_copy,
                     r_grp[:, part].rearrange("p (w j) -> p w j", j=PACK),
                     r_planess[u][:, part].rearrange("p (j w) -> p j w", j=PACK),
                 )
@@ -495,18 +484,23 @@ def tile_sub_graph_pb_t_kernel(tc, x_nodes, w1, b1, gamma, beta, w2, b2, out):
 
         for i in range(N_TILES + 6):
             load_x(i + LOAD_AHEAD)
-            normalise(i - 1)
+            if i - 2 < N_TILES - VECTOR_TILES:
+                reciprocal_deviation(i - 2)
+                normalise(nc.gpsimd, i - 2)
             add_bias(i)
             node_maxima(i - 6)
             negative_mean(i)
+            if i - 1 >= N_TILES - VECTOR_TILES:
+                reciprocal_deviation(i - 1)
+                normalise(nc.vector, i - 1)
             squared_deviations(i)
-            activate(i - 3, first=True)
-            reciprocal_deviation(i)
-            activate(i - 3, first=False)
             first_matmul(i + 1)
             second_matmul(i - 5)
+            transpose_n(i - 3)
+            activate(i - 3, first=True)
+            standard_deviation(i)
+            activate(i - 3, first=False)
             transpose_x(i + X_AHEAD)
-            transpose_n(i - 2)
             regroup_r(i - 4)
             quantise_x(i + 2)
             quantise_r(i - 4)

@@ -89,34 +89,35 @@ def tile_sub_graph_pb_t_kernel(tc, x_nodes, w1, b1, gamma, beta, w2, b2, out):
         nc.scalar.activation(out=warm[:], in_=warm[:], func=ACT.Sqrt)
         b1_row = const.tile([P, H], BF16)
         nc.vector.memset(b1_row[:], 0.0)
-        load_x(0)
         load_w1(0, 0)
         load_w1(1, 0)
-        load_x(1)
+        load_x(0)
         load_w1(0, 1)
+        load_x(1)
         load_w1(1, 1)
+        nc.sync.dma_start(out=b1_row[0:1, :], in_=b1.rearrange("(o h) -> o h", o=1))
         load_x(2)
-        nc.scalar.dma_start(out=b1_row[0:1, :], in_=b1.rearrange("(o h) -> o h", o=1))
-        gamma_raw = const.tile([P, PASSES, PACK], BF16)
-        nc.scalar.dma_start(
-            out=gamma_raw[:], in_=gamma.rearrange("(g p j) -> p g j", p=P, j=PACK)
-        )
-        beta_raw = const.tile([P, PASSES, PACK], BF16)
-        nc.scalar.dma_start(
-            out=beta_raw[:], in_=beta.rearrange("(g p j) -> p g j", p=P, j=PACK)
-        )
         w2_raw = const.tile([P, PASSES, PACK, G], BF16)
         nc.sync.dma_start(
             out=w2_raw[:], in_=w2.rearrange("(g p j) n -> p g j n", p=P, j=PACK)
         )
+        load_x(3)
+        gamma_raw = const.tile([P, PASSES, PACK], BF16)
+        nc.sync.dma_start(
+            out=gamma_raw[:], in_=gamma.rearrange("(g p j) -> p g j", p=P, j=PACK)
+        )
+        beta_raw = const.tile([P, PASSES, PACK], BF16)
+        nc.sync.dma_start(
+            out=beta_raw[:], in_=beta.rearrange("(g p j) -> p g j", p=P, j=PACK)
+        )
+        for i in range(4, LOAD_AHEAD):
+            load_x(i)
         b2_rows = const.tile([P, P], BF16)
         for cc in range(G_TILES):
-            nc.scalar.dma_start(
+            nc.sync.dma_start(
                 out=b2_rows[cc * LINES : (cc + 1) * LINES, :],
                 in_=b2[cc * P : (cc + 1) * P].partition_broadcast(LINES),
             )
-        for i in range(3, LOAD_AHEAD):
-            load_x(i)
 
         ident = const.tile([P, P], F32)
         make_identity(nc, ident[:])
@@ -453,9 +454,17 @@ def tile_sub_graph_pb_t_kernel(tc, x_nodes, w1, b1, gamma, beta, w2, b2, out):
         w2_codes = const.tile([P, PASSES, G], U32, align_bytes=64)
         w2_scales = const.tile([P, PASSES, G], U8, align_bytes=64)
 
-        def regroup_w2():
-            for g in range(PASSES):
-                regroup(nc.vector.tensor_copy, w2_grp[:, g, :, :], w2_raw[:, g, :, :])
+        def regroup_w2(g):
+            one = stat.tile([P, 1], F32, tag="one")
+            nc.vector.memset(one[:], 1.0)
+            nc.gpsimd.tensor_scalar(
+                out=w2_grp[:, g, :, :],
+                in0=w2_raw[:, g, :, :].rearrange("p t c -> p c t"),
+                scalar1=one[:],
+                scalar2=0.0,
+                op0=ALU.mult,
+                op1=ALU.add,
+            )
 
         def quantise_w2():
             nc.vector.quantize_mx(
@@ -464,29 +473,31 @@ def tile_sub_graph_pb_t_kernel(tc, x_nodes, w1, b1, gamma, beta, w2, b2, out):
                 in_=w2_grp[:].rearrange("p g c t -> p (g c t)"),
             )
 
-        transpose_x(0)
         regroup_w1(0, 0)
         regroup_w1(1, 0)
-        spread_b1(0)
-        transpose_x(1)
+        transpose_x(0)
         quantise_w1(0, 0)
-        quantise_x(0)
         quantise_w1(1, 0)
-        first_matmul(0, (0,))
         regroup_w1(0, 1)
+        transpose_x(1)
+        quantise_x(0)
         regroup_w1(1, 1)
+        spread_b1(0)
         spread_b1(1)
-        quantise_w1(0, 1)
-        quantise_x(1)
-        quantise_w1(1, 1)
-        first_matmul(0, (1,))
+        first_matmul(0, (0,))
         transpose_x(2)
+        quantise_w1(0, 1)
+        quantise_w1(1, 1)
+        quantise_x(1)
+        first_matmul(0, (1,))
 
         for i in range(N_TILES + 6):
             load_x(i + LOAD_AHEAD)
             if i - 2 < N_TILES - VECTOR_TILES:
                 reciprocal_deviation(i - 2)
                 normalise(nc.gpsimd, i - 2)
+            if i < PASSES:
+                regroup_w2(i)
             add_bias(i)
             node_maxima(i - 6)
             negative_mean(i)
@@ -495,18 +506,16 @@ def tile_sub_graph_pb_t_kernel(tc, x_nodes, w1, b1, gamma, beta, w2, b2, out):
                 normalise(nc.vector, i - 1)
             squared_deviations(i)
             first_matmul(i + 1)
-            second_matmul(i - 5)
             transpose_n(i - 3)
             activate(i - 3, first=True)
             standard_deviation(i)
             activate(i - 3, first=False)
             transpose_x(i + X_AHEAD)
+            second_matmul(i - 5)
             regroup_r(i - 4)
             quantise_x(i + 2)
             quantise_r(i - 4)
-            if i == 0:
-                regroup_w2()
-            if i == 1:
+            if i == 3:
                 quantise_w2()
 
         maxT_ps = psum.tile([P, P], F32, tag="xT", bufs=1)

from contextlib import ExitStack

import concourse.mybir as mybir
from concourse.masks import make_identity

F32 = mybir.dt.float32
BF16 = mybir.dt.bfloat16
U32 = mybir.dt.uint32
U8 = mybir.dt.uint8
FP8X4 = mybir.dt.float8_e4m3fn_x4
ACT = mybir.ActivationFunctionType
ALU = mybir.AluOpType
AX = mybir.AxisListType

P = 128
PACK = 4
K_PASS = P * PACK
BANK = 512

TOKENS = 64 * 64
NODES = 64
LINES = TOKENS // NODES
H = 1024
G = 256
EPS = 1e-5
PASSES = H // K_PASS
N_TILES = TOKENS // P
HALVES = H // BANK
G_TILES = G // P
PAIR = 2
N_PAIRS = N_TILES // PAIR
N_UNITS = N_TILES
VECTOR_TILES = 2

VECTOR_COLS = 352
X_AHEAD = 3
LOAD_AHEAD = 8

FLOPS = 2 * TOKENS * H * H + 2 * TOKENS * H * G


def regroup(copy, grouped, planes):
    copy(
        out=grouped.rearrange("p (c i) t -> p c t i", i=4),
        in_=planes.rearrange("p t (c i) -> p c t i", i=4),
    )


def tile_sub_graph_pb_t_kernel(tc, x_nodes, w1, b1, gamma, beta, w2, b2, out):
    nc = tc.nc
    x = x_nodes.rearrange("b l k -> (b l) k")

    with ExitStack() as ctx:
        const = ctx.enter_context(tc.tile_pool(name="const", bufs=1))
        wstage = ctx.enter_context(tc.tile_pool(name="wstage", bufs=4))
        xpool = ctx.enter_context(tc.tile_pool(name="xpool", bufs=3))
        hpool = ctx.enter_context(tc.tile_pool(name="hpool", bufs=6))
        stat = ctx.enter_context(tc.tile_pool(name="stat", bufs=6))
        rpool = ctx.enter_context(tc.tile_pool(name="rpool", bufs=2))
        psum = ctx.enter_context(tc.psum_pool(name="psum", bufs=1))
        ctx.enter_context(tc.manual_schedule())

        def in_range(i):
            return 0 <= i < N_TILES

        x_sbs = {}

        def load_x(i):
            if not in_range(i):
                return
            x_sb = xpool.tile([P, H], BF16, tag="x_sb", bufs=LOAD_AHEAD)
            nc.sync.dma_start(out=x_sb[:], in_=x[i * P : (i + 1) * P, :])
            x_sbs[i] = x_sb

        w1_raws = {}

        def load_w1(g, n):
            w1_raw = const.tile([P, PACK, BANK], BF16, name=f"w1_raw_{g}_{n}")
            nc.sync.dma_start(
                out=w1_raw[:],
                in_=w1[K_PASS * g : K_PASS * (g + 1), n * BANK : (n + 1) * BANK].rearrange(
                    "(p t) c -> p t c", t=PACK
                ),
            )
            w1_raws[(g, n)] = w1_raw

        warm = const.tile([P, 1], F32)
        nc.vector.memset(warm[:], 1.0)
        nc.scalar.activation(out=warm[:], in_=warm[:], func=ACT.Sqrt)
        b1_row = const.tile([P, H], BF16)
        nc.vector.memset(b1_row[:], 0.0)
        load_w1(0, 0)
        load_w1(1, 0)
        load_x(0)
        load_w1(0, 1)
        load_x(1)
        load_w1(1, 1)
        nc.sync.dma_start(out=b1_row[0:1, :], in_=b1.rearrange("(o h) -> o h", o=1))
        load_x(2)
        w2_raw = const.tile([P, PASSES, PACK, G], BF16)
        nc.sync.dma_start(
            out=w2_raw[:], in_=w2.rearrange("(g p j) n -> p g j n", p=P, j=PACK)
        )
        load_x(3)
        gamma_raw = const.tile([P, PASSES, PACK], BF16)
        nc.sync.dma_start(
            out=gamma_raw[:], in_=gamma.rearrange("(g p j) -> p g j", p=P, j=PACK)
        )
        beta_raw = const.tile([P, PASSES, PACK], BF16)
        nc.sync.dma_start(
            out=beta_raw[:], in_=beta.rearrange("(g p j) -> p g j", p=P, j=PACK)
        )
        for i in range(4, LOAD_AHEAD):
            load_x(i)
        b2_rows = const.tile([P, P], BF16)
        for cc in range(G_TILES):
            nc.sync.dma_start(
                out=b2_rows[cc * LINES : (cc + 1) * LINES, :],
                in_=b2[cc * P : (cc + 1) * P].partition_broadcast(LINES),
            )

        ident = const.tile([P, P], F32)
        make_identity(nc, ident[:])
        eps_col = const.tile([P, 1], F32)
        nc.gpsimd.tensor_scalar(
            out=eps_col[:], in0=ident[:, 0:1], scalar1=0.0, scalar2=EPS, op0=ALU.mult, op1=ALU.add
        )
        ones = const.tile([P, P], BF16)
        nc.vector.memset(ones[:], 1.0)
        gamma_col = const.tile([P, PASSES * PACK], F32)
        nc.gpsimd.tensor_copy(out=gamma_col[:], in_=gamma_raw[:].rearrange("p g j -> p (g j)"))
        beta_col = const.tile([P, PASSES * PACK], F32)
        nc.gpsimd.tensor_copy(out=beta_col[:], in_=beta_raw[:].rearrange("p g j -> p (g j)"))

        b1_all = const.tile([P, H], F32)

        def spread_b1(n):
            cols_n = slice(n * BANK, (n + 1) * BANK)
            b1_ps = psum.tile([P, BANK], F32, tag="h_ps", bufs=4)
            nc.tensor.matmul(
                out=b1_ps[:], lhsT=ones[:], rhs=b1_row[:, cols_n], start=True, stop=True
            )
            nc.scalar.copy(
                out=b1_all[:, cols_n].rearrange("p (j m) -> p j m", j=PACK),
                in_=b1_ps[:].rearrange("p (m j) -> p j m", j=PACK),
            )

        node_max = const.tile([P, G_TILES, LINES], F32)

        x_grps = {}
        x_mx = {}

        def transpose_x(i):
            if not in_range(i):
                return
            x_words = x_sbs[i][:].bitcast(F32)
            xT_ps = psum.tile([P, PASSES, 2, P], F32, tag="xT", bufs=1)
            for g in range(PASSES):
                for u in range(2):
                    w0 = g * 2 * P
                    nc.tensor.transpose(
                        xT_ps[:, g, u, :], x_words[:, w0 + u : w0 + 2 * P : 2], ident[:]
                    )
            x_grp = xpool.tile([P, H], BF16, tag="x_grp", align_bytes=64)
            nc.scalar.copy(
                out=x_grp[:].bitcast(F32).rearrange("p (g w u) -> p g w u", g=PASSES, u=2),
                in_=xT_ps[:].rearrange("p g u w -> p g w u"),
            )
            x_grps[i] = x_grp

        def quantise_x(i):
            if not in_range(i):
                return
            x_codes = xpool.tile([P, PASSES, P], U32, tag="x_codes", align_bytes=64)
            x_scales = xpool.tile([P, PASSES, P], U8, tag="x_scales", align_bytes=64)
            nc.vector.quantize_mx(
                out=x_codes[:].rearrange("p g w -> p (g w)").bitcast(FP8X4),
                scales=x_scales[:].rearrange("p g w -> p (g w)"),
                in_=x_grps[i][:],
            )
            x_mx[i] = (x_codes, x_scales)

        h_pss = {}
        h_sbs = {}
        h_sums = {}
        neg_means = {}
        sq_sums = {}

        def first_matmul(i, halves=range(HALVES)):
            if not in_range(i):
                return
            x_codes, x_scales = x_mx[i]
            for n in halves:
                cols_n = slice(n * BANK, (n + 1) * BANK)
                h_ps = psum.tile([P, BANK], F32, tag="h_ps", bufs=4)
                for g in range(PASSES):
                    nc.tensor.matmul_mx(
                        out=h_ps[:],
                        lhsT=x_codes[:, g, :].bitcast(FP8X4),
                        lhsT_scale=x_scales[:, g, :],
                        rhs=w1_codes[:, g, cols_n].bitcast(FP8X4),
                        rhs_scale=w1_scales[:, g, cols_n],
                        start=(g == 0),
                        stop=(g == PASSES - 1),
                    )
                h_pss[(i, n)] = h_ps

        def add_bias(i):
            if not in_range(i):
                return
            h_sb = hpool.tile([P, H], F32, tag="h_sb")
            h_sum = stat.tile([P, HALVES], F32, tag="h_sum")
            for n in range(HALVES):
                cols_n = slice(n * BANK, (n + 1) * BANK)
                nc.vector.scalar_tensor_tensor(
                    out=h_sb[:, cols_n].rearrange("p (j m) -> p j m", j=PACK),
                    in0=h_pss[(i, n)][:].rearrange("p (m j) -> p j m", j=PACK),
                    scalar=1.0,
                    in1=b1_all[:, cols_n].rearrange("p (j m) -> p j m", j=PACK),
                    op0=ALU.mult,
                    op1=ALU.add,
                    accum_out=h_sum[:, n : n + 1],
                )
            h_sbs[i] = h_sb
            h_sums[i] = h_sum

        def negative_mean(i):
            if not in_range(i):
                return
            neg_mean = stat.tile([P, 1], F32, tag="neg_mean")
            nc.vector.tensor_scalar(
                out=neg_mean[:],
                in0=h_sums[i][:, 0:1],
                scalar1=h_sums[i][:, 1:2],
                scalar2=-1.0 / H,
                op0=ALU.add,
                op1=ALU.mult,
            )
            neg_means[i] = neg_mean

        def squared_deviations(i):
            if not in_range(i):
                return
            sq_sum = stat.tile([P, 1], F32, tag="sq_sum")
            squares = hpool.tile([P, H], BF16, tag="squares", bufs=2)
            nc.scalar.activation(
                out=squares[:],
                in_=h_sbs[i][:],
                func=ACT.Square,
                bias=neg_means[i][:],
                scale=1.0,
                accum_out=sq_sum[:],
            )
            sq_sums[i] = sq_sum

        stds = {}
        rstds = {}

        def standard_deviation(i):
            if not in_range(i):
                return
            std = stat.tile([P, 1], F32, tag="std")
            nc.scalar.activation(
                out=std[:], in_=sq_sums[i][:], func=ACT.Sqrt, bias=eps_col[:], scale=1.0 / H
            )
            stds[i] = std

        def reciprocal_deviation(i):
            if not in_range(i):
                return
            rstd = stat.tile([P, 1], F32, tag="rstd")
            nc.vector.reciprocal(out=rstd[:], in_=stds[i][:])
            rstds[i] = rstd

        def normalise(engine, i):
            if not in_range(i):
                return
            engine.tensor_scalar(
                out=h_sbs[i][:],
                in0=h_sbs[i][:],
                scalar1=neg_means[i][:],
                scalar2=rstds[i][:],
                op0=ALU.add,
                op1=ALU.mult,
            )

        nT_pss = {}
        r_planess = {}
        r_grps = {}
        r_mx = {}


        def unit_in_range(u):
            return 0 <= u < N_UNITS

        def single(u):
            return u // PAIR == N_PAIRS - 1

        def unit_tiles(u):
            pair, part = divmod(u, PAIR)
            return [PAIR * pair + part] if single(u) else [PAIR * pair, PAIR * pair + 1]

        def unit_passes(u):
            return range(PASSES) if single(u) else [u % PASSES]

        def unit_chunks(u):
            return [PACK * g + j for g in unit_passes(u) for j in range(PACK)]

        def unit_width(u):
            return P * len(unit_tiles(u))

        def transpose_n(u):
            if not unit_in_range(u):
                return
            width = unit_width(u)
            per_bank = BANK // width
            for q, c in enumerate(unit_chunks(u)):
                if q % per_bank == 0:
                    tag, bufs = ("h_ps", 4) if single(u) else ("nT", 2)
                    nT_ps = psum.tile([P, BANK], F32, tag=tag, bufs=bufs)
                for part, i in enumerate(unit_tiles(u)):
                    col = (q % per_bank) * width + part * P
                    nc.tensor.transpose(
                        nT_ps[:, col : col + P], h_sbs[i][:, c * P : (c + 1) * P], ident[:]
                    )
                nT_pss[(u, q)] = nT_ps[:, (q % per_bank) * width : (q % per_bank + 1) * width]

        def activate(u, first):
            if not unit_in_range(u):
                return
            width = unit_width(u)
            if first:
                r_planes = rpool.tile([P, PACK * PAIR * P], BF16, tag="r_planes", bufs=3)
                r_planess[u] = r_planes
            for q, c in enumerate(unit_chunks(u)):
                if (q == 0) == first:
                    nc.scalar.activation(
                        out=r_planess[u][:, q * width : (q + 1) * width],
                        in_=nT_pss[(u, q)],
                        func=ACT.Relu,
                        bias=beta_col[:, c : c + 1],
                        scale=gamma_col[:, c : c + 1],
                    )

        def regroup_r(u):
            if not unit_in_range(u):
                return
            r_grp = rpool.tile([P, PACK * PAIR * P], BF16, tag="r_grp", align_bytes=64)
            size = PACK * unit_width(u)
            for k in range(len(unit_passes(u))):
                part = slice(k * size, (k + 1) * size)
                regroup(
                    nc.vector.tensor_copy,
                    r_grp[:, part].rearrange("p (w j) -> p w j", j=PACK),
                    r_planess[u][:, part].rearrange("p (j w) -> p j w", j=PACK),
                )
            r_grps[u] = r_grp

        def quantise_r(u):
            if not unit_in_range(u):
                return
            words = PAIR * P
            if single(u) or u % PASSES == 0:
                r_codes = rpool.tile([P, PASSES * words], U32, tag="r_codes", align_bytes=64)
                r_scales = rpool.tile([P, PASSES * words], U8, tag="r_scales", align_bytes=64)
                r_mx[u] = (r_codes, r_scales)
                cols = slice(0, words)
            else:
                r_mx[u] = r_mx[u - 1]
                cols = slice(words, 2 * words)
            r_codes, r_scales = r_mx[u]
            nc.vector.quantize_mx(
                out=r_codes[:, cols].bitcast(FP8X4),
                scales=r_scales[:, cols],
                in_=r_grps[u][:],
            )

        x1_pss = {}

        def x1_work(u):
            if not unit_in_range(u):
                return None
            pair, part = divmod(u, PAIR)
            if single(u):
                return ("tile", u), range(G_TILES), unit_tiles(u)
            if part == 1:
                chunks = [0] if pair < N_PAIRS - 2 else range(G_TILES)
                return ("pair", pair), chunks, unit_tiles(u)
            if pair > 0:
                return ("pair", pair - 1), [1], unit_tiles(u - 1)
            return None

        def second_matmul(u):
            work = x1_work(u)
            if work is None:
                return
            key, chunks, tiles = work
            if key not in x1_pss:
                tag, bufs = ("x1", 1) if len(tiles) == PAIR else ("nT", 2)
                x1_ps = psum.tile([P, G_TILES, PAIR * P], F32, tag=tag, bufs=bufs)
                x1_pss[key] = x1_ps
            r_codes, r_scales = r_mx[tiles[-1]]
            width = P * len(tiles)
            for cc in chunks:
                for g in range(PASSES):
                    words = slice(g * width, (g + 1) * width)
                    nc.tensor.matmul_mx(
                        out=x1_pss[key][:, cc, 0:width],
                        lhsT=w2_codes[:, g, cc * P : (cc + 1) * P].bitcast(FP8X4),
                        lhsT_scale=w2_scales[:, g, cc * P : (cc + 1) * P],
                        rhs=r_codes[:, words].bitcast(FP8X4),
                        rhs_scale=r_scales[:, words],
                        start=(g == 0),
                        stop=(g == PASSES - 1),
                    )

        def node_maxima(u):
            work = x1_work(u)
            if work is None:
                return
            key, chunks, tiles = work
            lines = P // NODES
            for cc in chunks:
                nc.vector.tensor_reduce(
                    out=node_max[:, cc, lines * tiles[0] : lines * (tiles[-1] + 1)],
                    in_=x1_pss[key][:, cc, 0 : P * len(tiles)].rearrange(
                        "p (q l) -> p q l", l=NODES
                    ),
                    axis=AX.X,
                    op=ALU.max,
                )

        w1_codes = const.tile([P, PASSES, H], U32, align_bytes=64)
        w1_scales = const.tile([P, PASSES, H], U8, align_bytes=64)
        w1_grps = {}

        def regroup_w1(g, n):
            w1_grp = wstage.tile([P, BANK, PACK], BF16, tag="w1_grp", align_bytes=64)
            w1_raw = w1_raws[(g, n)]
            mid = VECTOR_COLS
            regroup(nc.vector.tensor_copy, w1_grp[:, :mid, :], w1_raw[:, :, :mid])
            regroup(nc.scalar.copy, w1_grp[:, mid:, :], w1_raw[:, :, mid:])
            w1_grps[(g, n)] = w1_grp

        def quantise_w1(g, n):
            cols_n = slice(n * BANK, (n + 1) * BANK)
            nc.vector.quantize_mx(
                out=w1_codes[:, g, cols_n].bitcast(FP8X4),
                scales=w1_scales[:, g, cols_n],
                in_=w1_grps[(g, n)][:].rearrange("p c t -> p (c t)"),
            )

        w2_grp = const.tile([P, PASSES, G, PACK], BF16, align_bytes=64)
        w2_codes = const.tile([P, PASSES, G], U32, align_bytes=64)
        w2_scales = const.tile([P, PASSES, G], U8, align_bytes=64)

        def regroup_w2(g):
            one = stat.tile([P, 1], F32, tag="one")
            nc.vector.memset(one[:], 1.0)
            nc.gpsimd.tensor_scalar(
                out=w2_grp[:, g, :, :],
                in0=w2_raw[:, g, :, :].rearrange("p t c -> p c t"),
                scalar1=one[:],
                scalar2=0.0,
                op0=ALU.mult,
                op1=ALU.add,
            )

        def quantise_w2():
            nc.vector.quantize_mx(
                out=w2_codes[:].rearrange("p g c -> p (g c)").bitcast(FP8X4),
                scales=w2_scales[:].rearrange("p g c -> p (g c)"),
                in_=w2_grp[:].rearrange("p g c t -> p (g c t)"),
            )

        regroup_w1(0, 0)
        regroup_w1(1, 0)
        transpose_x(0)
        quantise_w1(0, 0)
        quantise_w1(1, 0)
        regroup_w1(0, 1)
        transpose_x(1)
        quantise_x(0)
        regroup_w1(1, 1)
        spread_b1(0)
        spread_b1(1)
        first_matmul(0, (0,))
        transpose_x(2)
        quantise_w1(0, 1)
        quantise_w1(1, 1)
        quantise_x(1)
        first_matmul(0, (1,))

        for i in range(N_TILES + 6):
            load_x(i + LOAD_AHEAD)
            if i - 2 < N_TILES - VECTOR_TILES:
                reciprocal_deviation(i - 2)
                normalise(nc.gpsimd, i - 2)
            if i < PASSES:
                regroup_w2(i)
            add_bias(i)
            node_maxima(i - 6)
            negative_mean(i)
            if i - 1 >= N_TILES - VECTOR_TILES:
                reciprocal_deviation(i - 1)
                normalise(nc.vector, i - 1)
            squared_deviations(i)
            first_matmul(i + 1)
            transpose_n(i - 3)
            activate(i - 3, first=True)
            standard_deviation(i)
            activate(i - 3, first=False)
            transpose_x(i + X_AHEAD)
            second_matmul(i - 5)
            regroup_r(i - 4)
            quantise_x(i + 2)
            quantise_r(i - 4)
            if i == 3:
                quantise_w2()

        maxT_ps = psum.tile([P, P], F32, tag="xT", bufs=1)
        nc.tensor.transpose(maxT_ps[:], node_max[:].rearrange("p c b -> p (c b)"), ident[:])
        result = const.tile([P, P], F32)
        nc.vector.tensor_tensor(out=result[:], in0=maxT_ps[:], in1=b2_rows[:], op=ALU.add)
        out_view = out.rearrange("b (r c j) -> r c b j", r=2, c=G_TILES)
        for r, queue in enumerate((nc.sync, nc.scalar)):
            for cc in range(G_TILES):
                queue.dma_start(out=out_view[r, cc], in_=result[cc * LINES : (cc + 1) * LINES, :])
